import numpy as np
import ml_dtypes


def mxq(x, axis, fmt="e4m3"):
    dtype, down = {"e4m3": (ml_dtypes.float8_e4m3fn, 7), "e5m2": (ml_dtypes.float8_e5m2, 14)}[fmt]
    v = np.moveaxis(np.asarray(x, np.float32).astype(ml_dtypes.bfloat16).astype(np.float64), axis, -1)
    blocks = v.reshape(v.shape[:-1] + (-1, 32))
    amax = np.abs(blocks).max(-1, keepdims=True)
    byte = np.maximum(np.where(amax > 0, np.frexp(amax)[1] - 1 + 127, 0) - down, 1)
    scale = np.exp2(byte - 127.0)
    codes = (blocks / scale).astype(np.float32).astype(dtype).astype(np.float64)
    return np.moveaxis((codes * scale).reshape(v.shape), -1, axis)


WIDE = False


def mx_kscale(k):
    if not WIDE:
        return np.ones(k)
    levels = np.array([10, -10, 5, -5, 0])
    a = np.random.permutation(np.resize(levels, k // 512 * 4)).reshape(k // 512, 4)
    idx = np.arange(k)
    return np.exp2(a[idx // 512, idx % 128 // 32])


BF16 = ml_dtypes.bfloat16


def bf(x):
    return np.asarray(x, np.float32).astype(BF16)


def f64(x):
    return np.asarray(x).astype(np.float64)


BATCH, IN_FEATURES, OUT_BY_WIN, WIN_SIZE, STRIDE = 256, 8192, 2, 64, 16
N_WIN = -(-IN_FEATURES // STRIDE)
OUT_FEATURES = N_WIN * OUT_BY_WIN


def build_mask():
    offset = WIN_SIZE // 2
    k = np.arange(N_WIN)
    lo = np.maximum(k * STRIDE - offset, 0)
    hi = k * STRIDE + WIN_SIZE - offset
    j = np.arange(IN_FEATURES)
    win_mask = (j[None, :] >= lo[:, None]) & (j[None, :] < hi[:, None])
    return np.repeat(win_mask, OUT_BY_WIN, axis=0).astype(np.float64)


def setup_inputs():
    s = mx_kscale(IN_FEATURES)
    mask = build_mask()
    bound = np.sqrt(3.0 / WIN_SIZE)
    W = np.random.uniform(-bound, bound, (OUT_FEATURES, IN_FEATURES)) * mask
    return {"x": bf(np.random.standard_normal((BATCH, IN_FEATURES)) * s), "W": bf(W / s[None, :]),
            "b": bf(np.random.uniform(-0.5, 0.5, OUT_FEATURES)), "mask": bf(mask)}


def reference(x, W, b, mask):
    return (mxq(f64(x), 1, "e4m3") @ mxq(f64(W), 1, "e4m3").T) + f64(b)

@@ -1,0 +1,156 @@
+from contextlib import ExitStack
+
+import concourse.mybir as mybir
+from concourse.masks import make_identity
+
+F32 = mybir.dt.float32
+BF16 = mybir.dt.bfloat16
+U32 = mybir.dt.uint32
+U8 = mybir.dt.uint8
+FP8X4 = mybir.dt.float8_e4m3fn_x4
+
+P = 128
+BATCH, FEATURES, OUTS = 256, 8192, 1024
+BATCH_TILES = BATCH // P
+K_PASS = 4 * P
+HALVES = 2
+PASSES = FEATURES // K_PASS
+PASSES_PER_CHUNK = 4
+CHUNKS = PASSES // PASSES_PER_CHUNK
+CHUNK_K = PASSES_PER_CHUNK * K_PASS
+BANK = 512
+
+WINDOW_STEP = 64
+PAD = 32
+LIVE_LO, LIVE_HI = PAD - 2, PAD + 68
+HOLD_BACK = 8
+
+FLOPS = 2 * BATCH * OUTS * 64
+BYTES = 2 * BATCH * FEATURES + 2 * OUTS * 64 + 2 * OUTS + 4 * BATCH * OUTS
+
+
+def quantise_chunk(nc, raw, identity, grouped_pool, planes_psum, codes, scales):
+    raw_words = raw[:].bitcast(F32)
+    grouped = grouped_pool.tile([P, CHUNK_K], BF16, align_bytes=64)
+    grouped_words = grouped[:].bitcast(F32).rearrange(
+        "p (i r u) -> p i r u", i=PASSES_PER_CHUNK, u=HALVES
+    )
+    passes_per_bank = BANK // (HALVES * P)
+    for bank in range(PASSES_PER_CHUNK // passes_per_bank):
+        first_pass = bank * passes_per_bank
+        planes = planes_psum.tile([P, passes_per_bank, HALVES, P], F32)
+        for i in range(passes_per_bank):
+            for u in range(HALVES):
+                first_word = ((first_pass + i) * HALVES + u) * P
+                nc.tensor.transpose(
+                    planes[:, i, u, :], raw_words[:, first_word : first_word + P], identity[:]
+                )
+        nc.scalar.copy(
+            out=grouped_words[:, first_pass : first_pass + passes_per_bank],
+            in_=planes[:].rearrange("p i u r -> p i r u"),
+        )
+    nc.vector.quantize_mx(out=codes[:].bitcast(FP8X4), scales=scales[:], in_=grouped[:])
+
+
+def tile_locallayer_k_kernel(tc, x, W, b, mask, out):
+    nc = tc.nc
+    with ExitStack() as ctx:
+        const = ctx.enter_context(tc.tile_pool(name="const", bufs=1))
+        x_raw_pool = ctx.enter_context(tc.tile_pool(name="x_raw", bufs=CHUNKS * BATCH_TILES))
+        w_raw_pool = ctx.enter_context(tc.tile_pool(name="w_raw", bufs=CHUNKS))
+        grouped_pool = ctx.enter_context(tc.tile_pool(name="grouped", bufs=3))
+        x_mx_pool = ctx.enter_context(tc.tile_pool(name="x_mx", bufs=3))
+        w_mx_pool = ctx.enter_context(tc.tile_pool(name="w_mx", bufs=2))
+        planes_psum = ctx.enter_context(tc.psum_pool(name="planes", bufs=4))
+        sums_psum = ctx.enter_context(tc.psum_pool(name="sums", bufs=3))
+
+        w_raw_chunks = []
+        x_raw_chunks = []
+        for g in range(CHUNKS):
+            w_raw = w_raw_pool.tile([P, CHUNK_K], BF16)
+            for i in range(PASSES_PER_CHUNK):
+                c = g * PASSES_PER_CHUNK + i
+                cols = slice(i * K_PASS, (i + 1) * K_PASS)
+                window_row = WINDOW_STEP * c - PAD
+                lo, hi = max(window_row, 0), min(window_row + P, OUTS)
+                if lo > window_row:
+                    nc.vector.memset(w_raw[0 : lo - window_row, cols], 0.0)
+                if hi < window_row + P:
+                    nc.vector.memset(w_raw[hi - window_row : P, cols], 0.0)
+                nc.sync.dma_start(
+                    out=w_raw[lo - window_row : hi - window_row, cols],
+                    in_=W[lo:hi, c * K_PASS : (c + 1) * K_PASS],
+                )
+            w_raw_chunks.append(w_raw)
+            for t in range(BATCH_TILES):
+                x_raw = x_raw_pool.tile([P, CHUNK_K], BF16)
+                nc.sync.dma_start(
+                    out=x_raw[:], in_=x[t * P : (t + 1) * P, g * CHUNK_K : (g + 1) * CHUNK_K]
+                )
+                x_raw_chunks.append(x_raw)
+
+        identity = const.tile([P, P], F32)
+        make_identity(nc, identity[:])
+
+        bias_rows = const.tile([P, OUTS], BF16)
+        nc.vector.memset(bias_rows[:], 0.0)
+        nc.scalar.dma_start(out=bias_rows[0:1, :], in_=b.unsqueeze(0))
+        ones = const.tile([P, P], BF16)
+        nc.vector.memset(ones[:], 1.0)
+        results = [
+            const.tile([P, PAD + OUTS + PAD], F32, name="result_%d" % t)
+            for t in range(BATCH_TILES)
+        ]
+        for t in range(BATCH_TILES):
+            nc.vector.memset(results[t][:, 0:PAD], 0.0)
+            nc.vector.memset(results[t][:, PAD + OUTS :], 0.0)
+        for first in range(0, OUTS, BANK):
+            sums = sums_psum.tile([P, BANK], F32)
+            nc.tensor.matmul(
+                out=sums[:], lhsT=ones[:], rhs=bias_rows[:, first : first + BANK],
+                start=True, stop=True,
+            )
+            for t in range(BATCH_TILES):
+                nc.scalar.copy(out=results[t][:, PAD + first : PAD + first + BANK], in_=sums[:])
+
+        stored = 0
+        for g in range(CHUNKS):
+            w_codes = w_mx_pool.tile([P, PASSES_PER_CHUNK * P], U32, align_bytes=64)
+            w_scales = w_mx_pool.tile([P, PASSES_PER_CHUNK * P], U8, align_bytes=64)
+            quantise_chunk(
+                nc, w_raw_chunks[g], identity, grouped_pool, planes_psum, w_codes, w_scales
+            )
+            complete = OUTS if g == CHUNKS - 1 else (g + 1) * PASSES_PER_CHUNK * WINDOW_STEP - HOLD_BACK
+            for t in range(BATCH_TILES):
+                x_codes = x_mx_pool.tile([P, PASSES_PER_CHUNK * P], U32, align_bytes=64)
+                x_scales = x_mx_pool.tile([P, PASSES_PER_CHUNK * P], U8, align_bytes=64)
+                quantise_chunk(
+                    nc, x_raw_chunks[g * BATCH_TILES + t], identity, grouped_pool, planes_psum,
+                    x_codes, x_scales,
+                )
+                sums = sums_psum.tile([P, BANK], F32)
+                for i in range(PASSES_PER_CHUNK):
+                    cols = slice(i * P, (i + 1) * P)
+                    nc.tensor.matmul_mx(
+                        out=sums[:, cols],
+                        lhsT=x_codes[:, cols].bitcast(FP8X4),
+                        lhsT_scale=x_scales[:, cols],
+                        rhs=w_codes[:, cols].bitcast(FP8X4),
+                        rhs_scale=w_scales[:, cols],
+                        start=True,
+                        stop=True,
+                    )
+                windows = sums[:].rearrange("p (j two n) -> p j two n", two=2, n=P)
+                for parity in range(2):
+                    first = (g * PASSES_PER_CHUNK + parity) * WINDOW_STEP
+                    target = results[t][:, first : first + BANK // 2].rearrange(
+                        "p (j n) -> p j n", n=P
+                    )[:, :, LIVE_LO:LIVE_HI]
+                    nc.vector.tensor_add(
+                        out=target, in0=windows[:, :, parity, LIVE_LO:LIVE_HI], in1=target
+                    )
+                nc.sync.dma_start(
+                    out=out[t * P : (t + 1) * P, stored:complete],
+                    in_=results[t][:, PAD + stored : PAD + complete],
+                )
+            stored = complete

@@ -13,7 +13,8 @@ P = 128
 BATCH, FEATURES, OUTS = 256, 8192, 1024
 BATCH_TILES = BATCH // P
 K_PASS = 4 * P
-HALVES = 2
+PLANES = 2
+PLANE_K = K_PASS // PLANES
 PASSES = FEATURES // K_PASS
 PASSES_PER_CHUNK = 4
 CHUNKS = PASSES // PASSES_PER_CHUNK
@@ -21,35 +22,25 @@ CHUNK_K = PASSES_PER_CHUNK * K_PASS
 BANK = 512
 
 WINDOW_STEP = 64
-PAD = 32
-LIVE_LO, LIVE_HI = PAD - 2, PAD + 68
+LEAD = 2
+LIVE = 70
+PLACED = 72
+PLANE_ROWS = P // PLANES
+PLANE_1_ROW = PLACED - PLANE_ROWS
+PLANE_1_SHIFT = PLANE_ROWS - PLANE_1_ROW
+ZERO_SHIFT = 40
 HOLD_BACK = 8
 
 FLOPS = 2 * BATCH * OUTS * 64
 BYTES = 2 * BATCH * FEATURES + 2 * OUTS * 64 + 2 * OUTS + 4 * BATCH * OUTS
 
 
-def quantise_chunk(nc, raw, identity, grouped_pool, planes_psum, codes, scales):
-    raw_words = raw[:].bitcast(F32)
-    grouped = grouped_pool.tile([P, CHUNK_K], BF16, align_bytes=64)
-    grouped_words = grouped[:].bitcast(F32).rearrange(
-        "p (i r u) -> p i r u", i=PASSES_PER_CHUNK, u=HALVES
-    )
-    passes_per_bank = BANK // (HALVES * P)
-    for bank in range(PASSES_PER_CHUNK // passes_per_bank):
-        first_pass = bank * passes_per_bank
-        planes = planes_psum.tile([P, passes_per_bank, HALVES, P], F32)
-        for i in range(passes_per_bank):
-            for u in range(HALVES):
-                first_word = ((first_pass + i) * HALVES + u) * P
-                nc.tensor.transpose(
-                    planes[:, i, u, :], raw_words[:, first_word : first_word + P], identity[:]
-                )
-        nc.scalar.copy(
-            out=grouped_words[:, first_pass : first_pass + passes_per_bank],
-            in_=planes[:].rearrange("p i u r -> p i r u"),
-        )
-    nc.vector.quantize_mx(out=codes[:].bitcast(FP8X4), scales=scales[:], in_=grouped[:])
+def diagonal_blocks(W, first_row, first_col, count):
+    block_step = WINDOW_STEP * FEATURES + K_PASS
+    start = first_row * FEATURES + first_col
+    flat = W.rearrange("o k -> (o k)")[start : start + count * block_step]
+    blocks = flat.rearrange("(j s) -> j s", s=block_step)[:, 0 : PLANE_ROWS * FEATURES]
+    return blocks.rearrange("j (r k) -> r j k", k=FEATURES)[:, :, 0:PLANE_K]
 
 
 def tile_locallayer_k_kernel(tc, x, W, b, mask, out):
@@ -57,37 +48,43 @@ def tile_locallayer_k_kernel(tc, x, W, b, mask, out):
     with ExitStack() as ctx:
         const = ctx.enter_context(tc.tile_pool(name="const", bufs=1))
         x_raw_pool = ctx.enter_context(tc.tile_pool(name="x_raw", bufs=CHUNKS * BATCH_TILES))
-        w_raw_pool = ctx.enter_context(tc.tile_pool(name="w_raw", bufs=CHUNKS))
-        grouped_pool = ctx.enter_context(tc.tile_pool(name="grouped", bufs=3))
-        x_mx_pool = ctx.enter_context(tc.tile_pool(name="x_mx", bufs=3))
-        w_mx_pool = ctx.enter_context(tc.tile_pool(name="w_mx", bufs=2))
-        planes_psum = ctx.enter_context(tc.psum_pool(name="planes", bufs=4))
+        grouped_pool = ctx.enter_context(tc.tile_pool(name="grouped", bufs=4))
+        x_mx_pool = ctx.enter_context(tc.tile_pool(name="x_mx", bufs=3 * BATCH_TILES))
+        planes_psum = ctx.enter_context(tc.psum_pool(name="planes", bufs=5))
         sums_psum = ctx.enter_context(tc.psum_pool(name="sums", bufs=3))
 
-        w_raw_chunks = []
-        x_raw_chunks = []
-        for g in range(CHUNKS):
-            w_raw = w_raw_pool.tile([P, CHUNK_K], BF16)
-            for i in range(PASSES_PER_CHUNK):
-                c = g * PASSES_PER_CHUNK + i
-                cols = slice(i * K_PASS, (i + 1) * K_PASS)
-                window_row = WINDOW_STEP * c - PAD
-                lo, hi = max(window_row, 0), min(window_row + P, OUTS)
-                if lo > window_row:
-                    nc.vector.memset(w_raw[0 : lo - window_row, cols], 0.0)
-                if hi < window_row + P:
-                    nc.vector.memset(w_raw[hi - window_row : P, cols], 0.0)
-                nc.sync.dma_start(
-                    out=w_raw[lo - window_row : hi - window_row, cols],
-                    in_=W[lo:hi, c * K_PASS : (c + 1) * K_PASS],
-                )
-            w_raw_chunks.append(w_raw)
+        def load_x_chunk(g):
+            tiles = []
             for t in range(BATCH_TILES):
                 x_raw = x_raw_pool.tile([P, CHUNK_K], BF16)
                 nc.sync.dma_start(
                     out=x_raw[:], in_=x[t * P : (t + 1) * P, g * CHUNK_K : (g + 1) * CHUNK_K]
                 )
-                x_raw_chunks.append(x_raw)
+                tiles.append(x_raw)
+            return tiles
+
+        x_raw_chunks = [load_x_chunk(0)]
+
+        w_raw = const.tile([P, PASSES, PLANE_K], BF16)
+        last = PASSES - 1
+        nc.vector.memset(w_raw[0:LEAD, 0, :], 0.0)
+        nc.vector.memset(w_raw[P - 32 : P, last, :], 0.0)
+        nc.sync.dma_start(out=w_raw[LEAD:PLANE_ROWS, 0, :], in_=W[0 : PLANE_ROWS - LEAD, 0:PLANE_K])
+        nc.sync.dma_start(
+            out=w_raw[0:PLANE_ROWS, 1:PASSES, :],
+            in_=diagonal_blocks(W, WINDOW_STEP - LEAD, K_PASS, last),
+        )
+        nc.sync.dma_start(
+            out=w_raw[PLANE_ROWS:P, 0:last, :],
+            in_=diagonal_blocks(W, PLANE_1_ROW - LEAD, PLANE_K, last),
+        )
+        last_row = WINDOW_STEP * last - LEAD + PLANE_1_ROW
+        nc.sync.dma_start(
+            out=w_raw[PLANE_ROWS : PLANE_ROWS + OUTS - last_row, last, :],
+            in_=W[last_row:OUTS, FEATURES - PLANE_K : FEATURES],
+        )
+        for g in range(1, CHUNKS):
+            x_raw_chunks.append(load_x_chunk(g))
 
         identity = const.tile([P, P], F32)
         make_identity(nc, identity[:])
@@ -97,13 +94,13 @@ def tile_locallayer_k_kernel(tc, x, W, b, mask, out):
         nc.scalar.dma_start(out=bias_rows[0:1, :], in_=b.unsqueeze(0))
         ones = const.tile([P, P], BF16)
         nc.vector.memset(ones[:], 1.0)
+        result_cols = WINDOW_STEP * last + P
         results = [
-            const.tile([P, PAD + OUTS + PAD], F32, name="result_%d" % t)
-            for t in range(BATCH_TILES)
+            const.tile([P, result_cols], F32, name="result_%d" % t) for t in range(BATCH_TILES)
         ]
         for t in range(BATCH_TILES):
-            nc.vector.memset(results[t][:, 0:PAD], 0.0)
-            nc.vector.memset(results[t][:, PAD + OUTS :], 0.0)
+            nc.vector.memset(results[t][:, 0:LEAD], 0.0)
+            nc.vector.memset(results[t][:, LEAD + OUTS :], 0.0)
         for first in range(0, OUTS, BANK):
             sums = sums_psum.tile([P, BANK], F32)
             nc.tensor.matmul(
@@ -111,46 +108,102 @@ def tile_locallayer_k_kernel(tc, x, W, b, mask, out):
                 start=True, stop=True,
             )
             for t in range(BATCH_TILES):
-                nc.scalar.copy(out=results[t][:, PAD + first : PAD + first + BANK], in_=sums[:])
+                nc.vector.tensor_copy(
+                    out=results[t][:, LEAD + first : LEAD + first + BANK], in_=sums[:]
+                )
 
+        def quantise_x_chunk(x_raw):
+            x_words = x_raw[:].bitcast(F32)
+            grouped = grouped_pool.tile([P, CHUNK_K], BF16, align_bytes=64)
+            grouped_words = grouped[:].bitcast(F32).rearrange(
+                "p (i r u) -> p i r u", i=PASSES_PER_CHUNK, u=PLANES
+            )
+            passes_per_bank = BANK // (PLANES * P)
+            for first_pass in range(0, PASSES_PER_CHUNK, passes_per_bank):
+                planes = planes_psum.tile([P, passes_per_bank, PLANES, P], F32, tag="planes")
+                for i in range(passes_per_bank):
+                    for u in range(PLANES):
+                        first_word = ((first_pass + i) * PLANES + u) * P
+                        nc.tensor.transpose(
+                            planes[:, i, u, :], x_words[:, first_word : first_word + P], identity[:]
+                        )
+                nc.scalar.copy(
+                    out=grouped_words[:, first_pass : first_pass + passes_per_bank],
+                    in_=planes[:].rearrange("p i u r -> p i r u"),
+                )
+            x_codes = x_mx_pool.tile([P, PASSES_PER_CHUNK * P], U32, align_bytes=64)
+            x_scales = x_mx_pool.tile([P, PASSES_PER_CHUNK * P], U8, align_bytes=64)
+            nc.vector.quantize_mx(out=x_codes[:].bitcast(FP8X4), scales=x_scales[:], in_=grouped[:])
+            return x_codes, x_scales
+
+        w_grouped = const.tile([P, PASSES * K_PASS], BF16, align_bytes=64)
+        w_codes = const.tile([P, PASSES * P], U32, align_bytes=64)
+        w_scales = const.tile([P, PASSES * P], U8, align_bytes=64)
+
+        def quantise_w():
+            w_words = w_raw[:].bitcast(F32)
+            w_grouped_words = w_grouped[:].bitcast(F32).rearrange(
+                "p (c n u) -> p c n u", c=PASSES, u=PLANES
+            )
+            nc.gpsimd.memset(w_grouped_words[:, :, PLACED:, :], 0.0)
+            for g in range(CHUNKS):
+                passes = slice(g * PASSES_PER_CHUNK, (g + 1) * PASSES_PER_CHUNK)
+                turned = planes_psum.tile([P, PASSES_PER_CHUNK, P], F32, tag="planes")
+                for i in range(PASSES_PER_CHUNK):
+                    nc.tensor.transpose(
+                        turned[:, i, :], w_words[:, g * PASSES_PER_CHUNK + i, :], identity[:]
+                    )
+                nc.scalar.copy(
+                    out=w_grouped_words[:, passes, 0:PLANE_1_SHIFT, :],
+                    in_=turned[:, :, 0 : PLANES * PLANE_1_SHIFT].rearrange(
+                        "p i (u n) -> p i n u", u=PLANES
+                    ),
+                )
+                nc.scalar.copy(
+                    out=w_grouped_words[:, passes, PLANE_1_SHIFT:PLACED, :],
+                    in_=turned[:, :, P - PLANES * ZERO_SHIFT : P].rearrange(
+                        "p i (u n) -> p i n u", u=PLANES
+                    )[:, :, ZERO_SHIFT - (PLACED - PLANE_1_SHIFT) : ZERO_SHIFT, :],
+                )
+                nc.vector.quantize_mx(
+                    out=w_codes[:, g * CHUNK_K // 4 : (g + 1) * CHUNK_K // 4].bitcast(FP8X4),
+                    scales=w_scales[:, g * CHUNK_K // 4 : (g + 1) * CHUNK_K // 4],
+                    in_=w_grouped[:, g * CHUNK_K : (g + 1) * CHUNK_K],
+                )
+
+        def multiply_chunk(g, t, x_codes, x_scales, stored, complete):
+            sums = sums_psum.tile([P, BANK], F32)
+            for i in range(PASSES_PER_CHUNK):
+                c = g * PASSES_PER_CHUNK + i
+                nc.tensor.matmul_mx(
+                    out=sums[:, i * P : (i + 1) * P],
+                    lhsT=x_codes[:, i * P : (i + 1) * P].bitcast(FP8X4),
+                    lhsT_scale=x_scales[:, i * P : (i + 1) * P],
+                    rhs=w_codes[:, c * P : (c + 1) * P].bitcast(FP8X4),
+                    rhs_scale=w_scales[:, c * P : (c + 1) * P],
+                    start=True,
+                    stop=True,
+                )
+            windows = sums[:].rearrange("p (j two n) -> p j two n", two=2, n=P)
+            for parity in range(2):
+                first = (g * PASSES_PER_CHUNK + parity) * WINDOW_STEP
+                target = results[t][:, first : first + BANK // 2].rearrange(
+                    "p (j n) -> p j n", n=P
+                )[:, :, 0:LIVE]
+                nc.vector.tensor_add(out=target, in0=windows[:, :, parity, 0:LIVE], in1=target)
+            nc.sync.dma_start(
+                out=out[t * P : (t + 1) * P, stored:complete],
+                in_=results[t][:, LEAD + stored : LEAD + complete],
+            )
+
+        ahead = [quantise_x_chunk(x_raw) for x_raw in x_raw_chunks[0]]
+        quantise_w()
         stored = 0
         for g in range(CHUNKS):
-            w_codes = w_mx_pool.tile([P, PASSES_PER_CHUNK * P], U32, align_bytes=64)
-            w_scales = w_mx_pool.tile([P, PASSES_PER_CHUNK * P], U8, align_bytes=64)
-            quantise_chunk(
-                nc, w_raw_chunks[g], identity, grouped_pool, planes_psum, w_codes, w_scales
-            )
+            ready = ahead
+            if g + 1 < CHUNKS:
+                ahead = [quantise_x_chunk(x_raw) for x_raw in x_raw_chunks[g + 1]]
             complete = OUTS if g == CHUNKS - 1 else (g + 1) * PASSES_PER_CHUNK * WINDOW_STEP - HOLD_BACK
             for t in range(BATCH_TILES):
-                x_codes = x_mx_pool.tile([P, PASSES_PER_CHUNK * P], U32, align_bytes=64)
-                x_scales = x_mx_pool.tile([P, PASSES_PER_CHUNK * P], U8, align_bytes=64)
-                quantise_chunk(
-                    nc, x_raw_chunks[g * BATCH_TILES + t], identity, grouped_pool, planes_psum,
-                    x_codes, x_scales,
-                )
-                sums = sums_psum.tile([P, BANK], F32)
-                for i in range(PASSES_PER_CHUNK):
-                    cols = slice(i * P, (i + 1) * P)
-                    nc.tensor.matmul_mx(
-                        out=sums[:, cols],
-                        lhsT=x_codes[:, cols].bitcast(FP8X4),
-                        lhsT_scale=x_scales[:, cols],
-                        rhs=w_codes[:, cols].bitcast(FP8X4),
-                        rhs_scale=w_scales[:, cols],
-                        start=True,
-                        stop=True,
-                    )
-                windows = sums[:].rearrange("p (j two n) -> p j two n", two=2, n=P)
-                for parity in range(2):
-                    first = (g * PASSES_PER_CHUNK + parity) * WINDOW_STEP
-                    target = results[t][:, first : first + BANK // 2].rearrange(
-                        "p (j n) -> p j n", n=P
-                    )[:, :, LIVE_LO:LIVE_HI]
-                    nc.vector.tensor_add(
-                        out=target, in0=windows[:, :, parity, LIVE_LO:LIVE_HI], in1=target
-                    )
-                nc.sync.dma_start(
-                    out=out[t * P : (t + 1) * P, stored:complete],
-                    in_=results[t][:, PAD + stored : PAD + complete],
-                )
+                multiply_chunk(g, t, ready[t][0], ready[t][1], stored, complete)
             stored = complete

@@ -7,6 +7,7 @@ F32 = mybir.dt.float32
 BF16 = mybir.dt.bfloat16
 U32 = mybir.dt.uint32
 U8 = mybir.dt.uint8
+I32 = mybir.dt.int32
 FP8X4 = mybir.dt.float8_e4m3fn_x4
 
 P = 128
@@ -31,6 +32,9 @@ PLANE_1_SHIFT = PLANE_ROWS - PLANE_1_ROW
 ZERO_SHIFT = 40
 HOLD_BACK = 8
 
+WARM_UP_PASSES = 6
+IDLE_PASSES = 2
+
 FLOPS = 2 * BATCH * OUTS * 64
 BYTES = 2 * BATCH * FEATURES + 2 * OUTS * 64 + 2 * OUTS + 4 * BATCH * OUTS
 
@@ -48,27 +52,68 @@ def tile_locallayer_k_kernel(tc, x, W, b, mask, out):
     with ExitStack() as ctx:
         const = ctx.enter_context(tc.tile_pool(name="const", bufs=1))
         x_raw_pool = ctx.enter_context(tc.tile_pool(name="x_raw", bufs=CHUNKS * BATCH_TILES))
-        grouped_pool = ctx.enter_context(tc.tile_pool(name="grouped", bufs=4))
-        x_mx_pool = ctx.enter_context(tc.tile_pool(name="x_mx", bufs=3 * BATCH_TILES))
-        planes_psum = ctx.enter_context(tc.psum_pool(name="planes", bufs=5))
+        grouped_pool = ctx.enter_context(tc.tile_pool(name="grouped", bufs=2 * BATCH_TILES))
+        x_mx_pool = ctx.enter_context(tc.tile_pool(name="x_mx", bufs=2 * BATCH_TILES))
+        planes_psum = ctx.enter_context(tc.psum_pool(name="planes", bufs=4))
         sums_psum = ctx.enter_context(tc.psum_pool(name="sums", bufs=3))
+        idle_psum = ctx.enter_context(tc.psum_pool(name="idle", bufs=1))
+        ctx.enter_context(tc.manual_schedule())
 
-        def load_x_chunk(g):
-            tiles = []
-            for t in range(BATCH_TILES):
-                x_raw = x_raw_pool.tile([P, CHUNK_K], BF16)
-                nc.sync.dma_start(
-                    out=x_raw[:], in_=x[t * P : (t + 1) * P, g * CHUNK_K : (g + 1) * CHUNK_K]
+        zeros = const.tile([P, 4 * BANK], BF16, align_bytes=64)
+        zero_codes = const.tile([P, BANK], U32, align_bytes=64)
+        zero_scales = const.tile([P, BANK], U8, align_bytes=64)
+        nc.vector.memset(zeros[:].bitcast(I32), 0)
+        nc.vector.quantize_mx(out=zero_codes[:].bitcast(FP8X4), scales=zero_scales[:], in_=zeros[:])
+        idle_sums = idle_psum.tile([P, BANK], F32)
+
+        def idle_passes(count):
+            for n in range(count):
+                nc.tensor.matmul_mx(
+                    out=idle_sums[:],
+                    lhsT=zero_codes[:, 0:P].bitcast(FP8X4),
+                    lhsT_scale=zero_scales[:, 0:P],
+                    rhs=zero_codes[:].bitcast(FP8X4),
+                    rhs_scale=zero_scales[:],
+                    start=True,
+                    stop=True,
                 )
-                tiles.append(x_raw)
-            return tiles
 
-        x_raw_chunks = [load_x_chunk(0)]
+        idle_passes(WARM_UP_PASSES)
 
+        identity = const.tile([P, P], F32)
+        make_identity(nc, identity[:])
+        bias_rows = const.tile([P, OUTS], BF16)
+        nc.vector.memset(bias_rows[:], 0.0)
+        ones = const.tile([P, P], BF16)
+        nc.vector.memset(ones[:], 1.0)
         w_raw = const.tile([P, PASSES, PLANE_K], BF16)
         last = PASSES - 1
         nc.vector.memset(w_raw[0:LEAD, 0, :], 0.0)
         nc.vector.memset(w_raw[P - 32 : P, last, :], 0.0)
+        result_cols = WINDOW_STEP * last + P
+        results = [
+            const.tile([P, result_cols], F32, name="result_%d" % t) for t in range(BATCH_TILES)
+        ]
+        for t in range(BATCH_TILES):
+            nc.vector.memset(results[t][:, 0:LEAD], 0.0)
+            nc.vector.memset(results[t][:, LEAD + OUTS :], 0.0)
+        w_grouped = const.tile([P, PASSES * K_PASS], BF16, align_bytes=64)
+        w_grouped_words = w_grouped[:].bitcast(F32).rearrange(
+            "p (c n u) -> p c n u", c=PASSES, u=PLANES
+        )
+        nc.gpsimd.memset(w_grouped_words[:, :, PLACED:, :], 0.0)
+        w_codes = const.tile([P, PASSES * P], U32, align_bytes=64)
+        w_scales = const.tile([P, PASSES * P], U8, align_bytes=64)
+
+        def load_x(g, t):
+            x_raw = x_raw_pool.tile([P, CHUNK_K], BF16)
+            nc.sync.dma_start(
+                out=x_raw[:], in_=x[t * P : (t + 1) * P, g * CHUNK_K : (g + 1) * CHUNK_K]
+            )
+            return x_raw
+
+        x_raw_chunks = [[load_x(0, t) for t in range(BATCH_TILES)]]
+        nc.sync.dma_start(out=bias_rows[0:1, :], in_=b.unsqueeze(0))
         nc.sync.dma_start(out=w_raw[LEAD:PLANE_ROWS, 0, :], in_=W[0 : PLANE_ROWS - LEAD, 0:PLANE_K])
         nc.sync.dma_start(
             out=w_raw[0:PLANE_ROWS, 1:PASSES, :],
@@ -84,35 +129,9 @@ def tile_locallayer_k_kernel(tc, x, W, b, mask, out):
             in_=W[last_row:OUTS, FEATURES - PLANE_K : FEATURES],
         )
         for g in range(1, CHUNKS):
-            x_raw_chunks.append(load_x_chunk(g))
+            x_raw_chunks.append([load_x(g, t) for t in range(BATCH_TILES)])
 
-        identity = const.tile([P, P], F32)
-        make_identity(nc, identity[:])
-
-        bias_rows = const.tile([P, OUTS], BF16)
-        nc.vector.memset(bias_rows[:], 0.0)
-        nc.scalar.dma_start(out=bias_rows[0:1, :], in_=b.unsqueeze(0))
-        ones = const.tile([P, P], BF16)
-        nc.vector.memset(ones[:], 1.0)
-        result_cols = WINDOW_STEP * last + P
-        results = [
-            const.tile([P, result_cols], F32, name="result_%d" % t) for t in range(BATCH_TILES)
-        ]
-        for t in range(BATCH_TILES):
-            nc.vector.memset(results[t][:, 0:LEAD], 0.0)
-            nc.vector.memset(results[t][:, LEAD + OUTS :], 0.0)
-        for first in range(0, OUTS, BANK):
-            sums = sums_psum.tile([P, BANK], F32)
-            nc.tensor.matmul(
-                out=sums[:], lhsT=ones[:], rhs=bias_rows[:, first : first + BANK],
-                start=True, stop=True,
-            )
-            for t in range(BATCH_TILES):
-                nc.vector.tensor_copy(
-                    out=results[t][:, LEAD + first : LEAD + first + BANK], in_=sums[:]
-                )
-
-        def quantise_x_chunk(x_raw):
+        def turn_x(x_raw):
             x_words = x_raw[:].bitcast(F32)
             grouped = grouped_pool.tile([P, CHUNK_K], BF16, align_bytes=64)
             grouped_words = grouped[:].bitcast(F32).rearrange(
@@ -131,47 +150,43 @@ def tile_locallayer_k_kernel(tc, x, W, b, mask, out):
                     out=grouped_words[:, first_pass : first_pass + passes_per_bank],
                     in_=planes[:].rearrange("p i u r -> p i r u"),
                 )
+            return grouped
+
+        def quantise_x(grouped):
             x_codes = x_mx_pool.tile([P, PASSES_PER_CHUNK * P], U32, align_bytes=64)
             x_scales = x_mx_pool.tile([P, PASSES_PER_CHUNK * P], U8, align_bytes=64)
             nc.vector.quantize_mx(out=x_codes[:].bitcast(FP8X4), scales=x_scales[:], in_=grouped[:])
             return x_codes, x_scales
 
-        w_grouped = const.tile([P, PASSES * K_PASS], BF16, align_bytes=64)
-        w_codes = const.tile([P, PASSES * P], U32, align_bytes=64)
-        w_scales = const.tile([P, PASSES * P], U8, align_bytes=64)
-
-        def quantise_w():
+        def turn_w(g):
             w_words = w_raw[:].bitcast(F32)
-            w_grouped_words = w_grouped[:].bitcast(F32).rearrange(
-                "p (c n u) -> p c n u", c=PASSES, u=PLANES
+            passes = slice(g * PASSES_PER_CHUNK, (g + 1) * PASSES_PER_CHUNK)
+            turned = planes_psum.tile([P, PASSES_PER_CHUNK, P], F32, tag="planes")
+            for i in range(PASSES_PER_CHUNK):
+                nc.tensor.transpose(
+                    turned[:, i, :], w_words[:, g * PASSES_PER_CHUNK + i, :], identity[:]
+                )
+            nc.scalar.copy(
+                out=w_grouped_words[:, passes, 0:PLANE_1_SHIFT, :],
+                in_=turned[:, :, 0 : PLANES * PLANE_1_SHIFT].rearrange(
+                    "p i (u n) -> p i n u", u=PLANES
+                ),
             )
-            nc.gpsimd.memset(w_grouped_words[:, :, PLACED:, :], 0.0)
-            for g in range(CHUNKS):
-                passes = slice(g * PASSES_PER_CHUNK, (g + 1) * PASSES_PER_CHUNK)
-                turned = planes_psum.tile([P, PASSES_PER_CHUNK, P], F32, tag="planes")
-                for i in range(PASSES_PER_CHUNK):
-                    nc.tensor.transpose(
-                        turned[:, i, :], w_words[:, g * PASSES_PER_CHUNK + i, :], identity[:]
-                    )
-                nc.scalar.copy(
-                    out=w_grouped_words[:, passes, 0:PLANE_1_SHIFT, :],
-                    in_=turned[:, :, 0 : PLANES * PLANE_1_SHIFT].rearrange(
-                        "p i (u n) -> p i n u", u=PLANES
-                    ),
-                )
-                nc.scalar.copy(
-                    out=w_grouped_words[:, passes, PLANE_1_SHIFT:PLACED, :],
-                    in_=turned[:, :, P - PLANES * ZERO_SHIFT : P].rearrange(
-                        "p i (u n) -> p i n u", u=PLANES
-                    )[:, :, ZERO_SHIFT - (PLACED - PLANE_1_SHIFT) : ZERO_SHIFT, :],
-                )
-                nc.vector.quantize_mx(
-                    out=w_codes[:, g * CHUNK_K // 4 : (g + 1) * CHUNK_K // 4].bitcast(FP8X4),
-                    scales=w_scales[:, g * CHUNK_K // 4 : (g + 1) * CHUNK_K // 4],
-                    in_=w_grouped[:, g * CHUNK_K : (g + 1) * CHUNK_K],
-                )
+            nc.scalar.copy(
+                out=w_grouped_words[:, passes, PLANE_1_SHIFT:PLACED, :],
+                in_=turned[:, :, P - PLANES * ZERO_SHIFT : P].rearrange(
+                    "p i (u n) -> p i n u", u=PLANES
+                )[:, :, ZERO_SHIFT - (PLACED - PLANE_1_SHIFT) : ZERO_SHIFT, :],
+            )
 
-        def multiply_chunk(g, t, x_codes, x_scales, stored, complete):
+        def quantise_w(g):
+            nc.vector.quantize_mx(
+                out=w_codes[:, g * CHUNK_K // 4 : (g + 1) * CHUNK_K // 4].bitcast(FP8X4),
+                scales=w_scales[:, g * CHUNK_K // 4 : (g + 1) * CHUNK_K // 4],
+                in_=w_grouped[:, g * CHUNK_K : (g + 1) * CHUNK_K],
+            )
+
+        def multiply(g, x_codes, x_scales):
             sums = sums_psum.tile([P, BANK], F32)
             for i in range(PASSES_PER_CHUNK):
                 c = g * PASSES_PER_CHUNK + i
@@ -184,6 +199,9 @@ def tile_locallayer_k_kernel(tc, x, W, b, mask, out):
                     start=True,
                     stop=True,
                 )
+            return sums
+
+        def add_and_store(g, t, sums):
             windows = sums[:].rearrange("p (j two n) -> p j two n", two=2, n=P)
             for parity in range(2):
                 first = (g * PASSES_PER_CHUNK + parity) * WINDOW_STEP
@@ -191,19 +209,45 @@ def tile_locallayer_k_kernel(tc, x, W, b, mask, out):
                     "p (j n) -> p j n", n=P
                 )[:, :, 0:LIVE]
                 nc.vector.tensor_add(out=target, in0=windows[:, :, parity, 0:LIVE], in1=target)
+            chunk_outs = PASSES_PER_CHUNK * WINDOW_STEP
+            stored = max(g * chunk_outs - HOLD_BACK, 0)
+            complete = OUTS if g == CHUNKS - 1 else (g + 1) * chunk_outs - HOLD_BACK
             nc.sync.dma_start(
                 out=out[t * P : (t + 1) * P, stored:complete],
                 in_=results[t][:, LEAD + stored : LEAD + complete],
             )
 
-        ahead = [quantise_x_chunk(x_raw) for x_raw in x_raw_chunks[0]]
-        quantise_w()
-        stored = 0
+        grouped_ahead = [turn_x(x_raw) for x_raw in x_raw_chunks[0]]
+        idle_passes(IDLE_PASSES)
+        ahead = [quantise_x(grouped) for grouped in grouped_ahead]
+
+        for first in range(0, OUTS, BANK):
+            sums = sums_psum.tile([P, BANK], F32)
+            nc.tensor.matmul(
+                out=sums[:], lhsT=ones[:], rhs=bias_rows[:, first : first + BANK],
+                start=True, stop=True,
+            )
+            for t in range(BATCH_TILES):
+                nc.vector.tensor_copy(
+                    out=results[t][:, LEAD + first : LEAD + first + BANK], in_=sums[:]
+                )
+
+        for g in range(CHUNKS):
+            turn_w(g)
+        idle_passes(IDLE_PASSES)
+        for g in range(CHUNKS):
+            quantise_w(g)
+
         for g in range(CHUNKS):
             ready = ahead
-            if g + 1 < CHUNKS:
-                ahead = [quantise_x_chunk(x_raw) for x_raw in x_raw_chunks[g + 1]]
-            complete = OUTS if g == CHUNKS - 1 else (g + 1) * PASSES_PER_CHUNK * WINDOW_STEP - HOLD_BACK
+            more = g + 1 < CHUNKS
+            if more:
+                grouped_ahead = [turn_x(x_raw) for x_raw in x_raw_chunks[g + 1]]
+            sums_ready = [multiply(g, ready[t][0], ready[t][1]) for t in range(BATCH_TILES)]
+            if more:
+                idle_passes(IDLE_PASSES)
+                ahead = []
             for t in range(BATCH_TILES):
-                multiply_chunk(g, t, ready[t][0], ready[t][1], stored, complete)
-            stored = complete
+                if more:
+                    ahead.append(quantise_x(grouped_ahead[t]))
+                add_and_store(g, t, sums_ready[t])

@@ -7,7 +7,6 @@ F32 = mybir.dt.float32
 BF16 = mybir.dt.bfloat16
 U32 = mybir.dt.uint32
 U8 = mybir.dt.uint8
-I32 = mybir.dt.int32
 FP8X4 = mybir.dt.float8_e4m3fn_x4
 
 P = 128
@@ -32,8 +31,6 @@ PLANE_1_SHIFT = PLANE_ROWS - PLANE_1_ROW
 ZERO_SHIFT = 40
 HOLD_BACK = 8
 
-WARM_UP_PASSES = 6
-IDLE_PASSES = 2
 
 FLOPS = 2 * BATCH * OUTS * 64
 BYTES = 2 * BATCH * FEATURES + 2 * OUTS * 64 + 2 * OUTS + 4 * BATCH * OUTS
@@ -56,29 +53,7 @@ def tile_locallayer_k_kernel(tc, x, W, b, mask, out):
         x_mx_pool = ctx.enter_context(tc.tile_pool(name="x_mx", bufs=2 * BATCH_TILES))
         planes_psum = ctx.enter_context(tc.psum_pool(name="planes", bufs=4))
         sums_psum = ctx.enter_context(tc.psum_pool(name="sums", bufs=3))
-        idle_psum = ctx.enter_context(tc.psum_pool(name="idle", bufs=1))
         ctx.enter_context(tc.manual_schedule())
-
-        zeros = const.tile([P, 4 * BANK], BF16, align_bytes=64)
-        zero_codes = const.tile([P, BANK], U32, align_bytes=64)
-        zero_scales = const.tile([P, BANK], U8, align_bytes=64)
-        nc.vector.memset(zeros[:].bitcast(I32), 0)
-        nc.vector.quantize_mx(out=zero_codes[:].bitcast(FP8X4), scales=zero_scales[:], in_=zeros[:])
-        idle_sums = idle_psum.tile([P, BANK], F32)
-
-        def idle_passes(count):
-            for n in range(count):
-                nc.tensor.matmul_mx(
-                    out=idle_sums[:],
-                    lhsT=zero_codes[:, 0:P].bitcast(FP8X4),
-                    lhsT_scale=zero_scales[:, 0:P],
-                    rhs=zero_codes[:].bitcast(FP8X4),
-                    rhs_scale=zero_scales[:],
-                    start=True,
-                    stop=True,
-                )
-
-        idle_passes(WARM_UP_PASSES)
 
         identity = const.tile([P, P], F32)
         make_identity(nc, identity[:])
@@ -218,7 +193,6 @@ def tile_locallayer_k_kernel(tc, x, W, b, mask, out):
             )
 
         grouped_ahead = [turn_x(x_raw) for x_raw in x_raw_chunks[0]]
-        idle_passes(IDLE_PASSES)
         ahead = [quantise_x(grouped) for grouped in grouped_ahead]
 
         for first in range(0, OUTS, BANK):
@@ -234,7 +208,6 @@ def tile_locallayer_k_kernel(tc, x, W, b, mask, out):
 
         for g in range(CHUNKS):
             turn_w(g)
-        idle_passes(IDLE_PASSES)
         for g in range(CHUNKS):
             quantise_w(g)
 
@@ -245,7 +218,6 @@ def tile_locallayer_k_kernel(tc, x, W, b, mask, out):
                 grouped_ahead = [turn_x(x_raw) for x_raw in x_raw_chunks[g + 1]]
             sums_ready = [multiply(g, ready[t][0], ready[t][1]) for t in range(BATCH_TILES)]
             if more:
-                idle_passes(IDLE_PASSES)
                 ahead = []
             for t in range(BATCH_TILES):
                 if more:

@@ -7,6 +7,7 @@ F32 = mybir.dt.float32
 BF16 = mybir.dt.bfloat16
 U32 = mybir.dt.uint32
 U8 = mybir.dt.uint8
+I32 = mybir.dt.int32
 FP8X4 = mybir.dt.float8_e4m3fn_x4
 
 P = 128
@@ -51,14 +52,14 @@ def tile_locallayer_k_kernel(tc, x, W, b, mask, out):
         x_raw_pool = ctx.enter_context(tc.tile_pool(name="x_raw", bufs=CHUNKS * BATCH_TILES))
         grouped_pool = ctx.enter_context(tc.tile_pool(name="grouped", bufs=2 * BATCH_TILES))
         x_mx_pool = ctx.enter_context(tc.tile_pool(name="x_mx", bufs=2 * BATCH_TILES))
-        planes_psum = ctx.enter_context(tc.psum_pool(name="planes", bufs=4))
+        planes_psum = ctx.enter_context(tc.psum_pool(name="planes", bufs=5))
         sums_psum = ctx.enter_context(tc.psum_pool(name="sums", bufs=3))
         ctx.enter_context(tc.manual_schedule())
 
         identity = const.tile([P, P], F32)
         make_identity(nc, identity[:])
         bias_rows = const.tile([P, OUTS], BF16)
-        nc.vector.memset(bias_rows[:], 0.0)
+        nc.vector.memset(bias_rows[:].bitcast(I32), 0)
         ones = const.tile([P, P], BF16)
         nc.vector.memset(ones[:], 1.0)
         w_raw = const.tile([P, PASSES, PLANE_K], BF16)
@@ -82,28 +83,43 @@ def tile_locallayer_k_kernel(tc, x, W, b, mask, out):
 
         def load_x(g, t):
             x_raw = x_raw_pool.tile([P, CHUNK_K], BF16)
-            nc.sync.dma_start(
-                out=x_raw[:], in_=x[t * P : (t + 1) * P, g * CHUNK_K : (g + 1) * CHUNK_K]
-            )
+            for first in range(0, CHUNK_K, CHUNK_K // 2):
+                nc.sync.dma_start(
+                    out=x_raw[:, first : first + CHUNK_K // 2],
+                    in_=x[t * P : (t + 1) * P, g * CHUNK_K + first : g * CHUNK_K + first + CHUNK_K // 2],
+                )
             return x_raw
 
-        x_raw_chunks = [[load_x(0, t) for t in range(BATCH_TILES)]]
+        def load_w(g):
+            first = g * PASSES_PER_CHUNK
+            if g == 0:
+                nc.sync.dma_start(
+                    out=w_raw[LEAD:PLANE_ROWS, 0, :], in_=W[0 : PLANE_ROWS - LEAD, 0:PLANE_K]
+                )
+            if g == CHUNKS - 1:
+                last_row = WINDOW_STEP * last - LEAD + PLANE_1_ROW
+                nc.sync.dma_start(
+                    out=w_raw[PLANE_ROWS : PLANE_ROWS + OUTS - last_row, last, :],
+                    in_=W[last_row:OUTS, FEATURES - PLANE_K : FEATURES],
+                )
+            for u in range(PLANES):
+                lo = max(first, 1) if u == 0 else first
+                hi = first + PASSES_PER_CHUNK if u == 0 else min(first + PASSES_PER_CHUNK, last)
+                nc.sync.dma_start(
+                    out=w_raw[u * PLANE_ROWS : (u + 1) * PLANE_ROWS, lo:hi, :],
+                    in_=diagonal_blocks(
+                        W,
+                        WINDOW_STEP * lo - LEAD + u * PLANE_1_ROW,
+                        K_PASS * lo + u * PLANE_K,
+                        hi - lo,
+                    ),
+                )
+
         nc.sync.dma_start(out=bias_rows[0:1, :], in_=b.unsqueeze(0))
-        nc.sync.dma_start(out=w_raw[LEAD:PLANE_ROWS, 0, :], in_=W[0 : PLANE_ROWS - LEAD, 0:PLANE_K])
-        nc.sync.dma_start(
-            out=w_raw[0:PLANE_ROWS, 1:PASSES, :],
-            in_=diagonal_blocks(W, WINDOW_STEP - LEAD, K_PASS, last),
-        )
-        nc.sync.dma_start(
-            out=w_raw[PLANE_ROWS:P, 0:last, :],
-            in_=diagonal_blocks(W, PLANE_1_ROW - LEAD, PLANE_K, last),
-        )
-        last_row = WINDOW_STEP * last - LEAD + PLANE_1_ROW
-        nc.sync.dma_start(
-            out=w_raw[PLANE_ROWS : PLANE_ROWS + OUTS - last_row, last, :],
-            in_=W[last_row:OUTS, FEATURES - PLANE_K : FEATURES],
-        )
+        x_raw_chunks = [[load_x(0, t) for t in range(BATCH_TILES)]]
+        load_w(0)
         for g in range(1, CHUNKS):
+            load_w(g)
             x_raw_chunks.append([load_x(g, t) for t in range(BATCH_TILES)])
 
         def turn_x(x_raw):
@@ -192,9 +208,6 @@ def tile_locallayer_k_kernel(tc, x, W, b, mask, out):
                 in_=results[t][:, LEAD + stored : LEAD + complete],
             )
 
-        grouped_ahead = [turn_x(x_raw) for x_raw in x_raw_chunks[0]]
-        ahead = [quantise_x(grouped) for grouped in grouped_ahead]
-
         for first in range(0, OUTS, BANK):
             sums = sums_psum.tile([P, BANK], F32)
             nc.tensor.matmul(
@@ -206,19 +219,20 @@ def tile_locallayer_k_kernel(tc, x, W, b, mask, out):
                     out=results[t][:, LEAD + first : LEAD + first + BANK], in_=sums[:]
                 )
 
-        for g in range(CHUNKS):
-            turn_w(g)
-        for g in range(CHUNKS):
-            quantise_w(g)
+        grouped_ahead = [turn_x(x_raw) for x_raw in x_raw_chunks[0]]
+        ahead = [quantise_x(grouped) for grouped in grouped_ahead]
+        turn_w(0)
+        quantise_w(0)
 
         for g in range(CHUNKS):
             ready = ahead
             more = g + 1 < CHUNKS
             if more:
+                turn_w(g + 1)
                 grouped_ahead = [turn_x(x_raw) for x_raw in x_raw_chunks[g + 1]]
-            sums_ready = [multiply(g, ready[t][0], ready[t][1]) for t in range(BATCH_TILES)]
-            if more:
+                quantise_w(g + 1)
                 ahead = []
+            sums_ready = [multiply(g, ready[t][0], ready[t][1]) for t in range(BATCH_TILES)]
             for t in range(BATCH_TILES):
                 if more:
                     ahead.append(quantise_x(grouped_ahead[t]))

@@ -32,6 +32,9 @@ PLANE_1_SHIFT = PLANE_ROWS - PLANE_1_ROW
 ZERO_SHIFT = 40
 HOLD_BACK = 8
 
+UNITS = [(first, PASSES_PER_CHUNK) for first in range(0, PASSES - PASSES_PER_CHUNK, PASSES_PER_CHUNK)]
+UNITS = UNITS + [(PASSES - 4, 2), (PASSES - 2, 1), (PASSES - 1, 1)]
+
 
 FLOPS = 2 * BATCH * OUTS * 64
 BYTES = 2 * BATCH * FEATURES + 2 * OUTS * 64 + 2 * OUTS + 4 * BATCH * OUTS
@@ -49,7 +52,7 @@ def tile_locallayer_k_kernel(tc, x, W, b, mask, out):
     nc = tc.nc
     with ExitStack() as ctx:
         const = ctx.enter_context(tc.tile_pool(name="const", bufs=1))
-        x_raw_pool = ctx.enter_context(tc.tile_pool(name="x_raw", bufs=CHUNKS * BATCH_TILES))
+        x_raw_pool = ctx.enter_context(tc.tile_pool(name="x_raw", bufs=len(UNITS) * BATCH_TILES))
         grouped_pool = ctx.enter_context(tc.tile_pool(name="grouped", bufs=2 * BATCH_TILES))
         x_mx_pool = ctx.enter_context(tc.tile_pool(name="x_mx", bufs=2 * BATCH_TILES))
         planes_psum = ctx.enter_context(tc.psum_pool(name="planes", bufs=5))
@@ -81,12 +84,13 @@ def tile_locallayer_k_kernel(tc, x, W, b, mask, out):
         w_codes = const.tile([P, PASSES * P], U32, align_bytes=64)
         w_scales = const.tile([P, PASSES * P], U8, align_bytes=64)
 
-        def load_x(g, t):
+        def load_x(first_pass, count, t):
             x_raw = x_raw_pool.tile([P, CHUNK_K], BF16)
-            for first in range(0, CHUNK_K, CHUNK_K // 2):
+            for i in range(0, count, 2):
+                here = min(2, count - i)
                 nc.sync.dma_start(
-                    out=x_raw[:, first : first + CHUNK_K // 2],
-                    in_=x[t * P : (t + 1) * P, g * CHUNK_K + first : g * CHUNK_K + first + CHUNK_K // 2],
+                    out=x_raw[:, i * K_PASS : (i + here) * K_PASS],
+                    in_=x[t * P : (t + 1) * P, (first_pass + i) * K_PASS : (first_pass + i + here) * K_PASS],
                 )
             return x_raw
 
@@ -116,37 +120,44 @@ def tile_locallayer_k_kernel(tc, x, W, b, mask, out):
                 )
 
         nc.sync.dma_start(out=bias_rows[0:1, :], in_=b.unsqueeze(0))
-        x_raw_chunks = [[load_x(0, t) for t in range(BATCH_TILES)]]
-        load_w(0)
-        for g in range(1, CHUNKS):
-            load_w(g)
-            x_raw_chunks.append([load_x(g, t) for t in range(BATCH_TILES)])
+        x_raw_units = []
+        for first_pass, count in UNITS:
+            if first_pass % PASSES_PER_CHUNK == 0 and first_pass > 0:
+                load_w(first_pass // PASSES_PER_CHUNK)
+            x_raw_units.append([load_x(first_pass, count, t) for t in range(BATCH_TILES)])
+            if first_pass == 0:
+                load_w(0)
 
-        def turn_x(x_raw):
+        def turn_x(x_raw, count):
             x_words = x_raw[:].bitcast(F32)
             grouped = grouped_pool.tile([P, CHUNK_K], BF16, align_bytes=64)
             grouped_words = grouped[:].bitcast(F32).rearrange(
                 "p (i r u) -> p i r u", i=PASSES_PER_CHUNK, u=PLANES
             )
             passes_per_bank = BANK // (PLANES * P)
-            for first_pass in range(0, PASSES_PER_CHUNK, passes_per_bank):
+            for first in range(0, count, passes_per_bank):
+                here = min(passes_per_bank, count - first)
                 planes = planes_psum.tile([P, passes_per_bank, PLANES, P], F32, tag="planes")
-                for i in range(passes_per_bank):
+                for i in range(here):
                     for u in range(PLANES):
-                        first_word = ((first_pass + i) * PLANES + u) * P
+                        first_word = ((first + i) * PLANES + u) * P
                         nc.tensor.transpose(
                             planes[:, i, u, :], x_words[:, first_word : first_word + P], identity[:]
                         )
                 nc.scalar.copy(
-                    out=grouped_words[:, first_pass : first_pass + passes_per_bank],
-                    in_=planes[:].rearrange("p i u r -> p i r u"),
+                    out=grouped_words[:, first : first + here],
+                    in_=planes[:, 0:here].rearrange("p i u r -> p i r u"),
                 )
             return grouped
 
-        def quantise_x(grouped):
+        def quantise_x(grouped, count):
             x_codes = x_mx_pool.tile([P, PASSES_PER_CHUNK * P], U32, align_bytes=64)
             x_scales = x_mx_pool.tile([P, PASSES_PER_CHUNK * P], U8, align_bytes=64)
-            nc.vector.quantize_mx(out=x_codes[:].bitcast(FP8X4), scales=x_scales[:], in_=grouped[:])
+            nc.vector.quantize_mx(
+                out=x_codes[:, 0 : count * P].bitcast(FP8X4),
+                scales=x_scales[:, 0 : count * P],
+                in_=grouped[:, 0 : count * K_PASS],
+            )
             return x_codes, x_scales
 
         def turn_w(g):
@@ -177,10 +188,10 @@ def tile_locallayer_k_kernel(tc, x, W, b, mask, out):
                 in_=w_grouped[:, g * CHUNK_K : (g + 1) * CHUNK_K],
             )
 
-        def multiply(g, x_codes, x_scales):
+        def multiply(first_pass, count, x_codes, x_scales):
             sums = sums_psum.tile([P, BANK], F32)
-            for i in range(PASSES_PER_CHUNK):
-                c = g * PASSES_PER_CHUNK + i
+            for i in range(count):
+                c = first_pass + i
                 nc.tensor.matmul_mx(
                     out=sums[:, i * P : (i + 1) * P],
                     lhsT=x_codes[:, i * P : (i + 1) * P].bitcast(FP8X4),
@@ -192,17 +203,20 @@ def tile_locallayer_k_kernel(tc, x, W, b, mask, out):
                 )
             return sums
 
-        def add_and_store(g, t, sums):
+        def add_and_store(first_pass, count, t, sums):
             windows = sums[:].rearrange("p (j two n) -> p j two n", two=2, n=P)
-            for parity in range(2):
-                first = (g * PASSES_PER_CHUNK + parity) * WINDOW_STEP
-                target = results[t][:, first : first + BANK // 2].rearrange(
+            for parity in range(min(2, count)):
+                pairs = (count + 1) // 2
+                start = (first_pass + parity) * WINDOW_STEP
+                target = results[t][:, start : start + pairs * P].rearrange(
                     "p (j n) -> p j n", n=P
                 )[:, :, 0:LIVE]
-                nc.vector.tensor_add(out=target, in0=windows[:, :, parity, 0:LIVE], in1=target)
-            chunk_outs = PASSES_PER_CHUNK * WINDOW_STEP
-            stored = max(g * chunk_outs - HOLD_BACK, 0)
-            complete = OUTS if g == CHUNKS - 1 else (g + 1) * chunk_outs - HOLD_BACK
+                nc.vector.tensor_add(
+                    out=target, in0=windows[:, 0:pairs, parity, 0:LIVE], in1=target
+                )
+            stored = max(first_pass * WINDOW_STEP - HOLD_BACK, 0)
+            after = first_pass + count
+            complete = OUTS if after == PASSES else after * WINDOW_STEP - HOLD_BACK
             nc.sync.dma_start(
                 out=out[t * P : (t + 1) * P, stored:complete],
                 in_=results[t][:, LEAD + stored : LEAD + complete],
@@ -219,21 +233,28 @@ def tile_locallayer_k_kernel(tc, x, W, b, mask, out):
                     out=results[t][:, LEAD + first : LEAD + first + BANK], in_=sums[:]
                 )
 
-        grouped_ahead = [turn_x(x_raw) for x_raw in x_raw_chunks[0]]
-        ahead = [quantise_x(grouped) for grouped in grouped_ahead]
+        grouped_ahead = [turn_x(x_raw, UNITS[0][1]) for x_raw in x_raw_units[0]]
+        ahead = [quantise_x(grouped, UNITS[0][1]) for grouped in grouped_ahead]
         turn_w(0)
         quantise_w(0)
 
-        for g in range(CHUNKS):
+        for n in range(len(UNITS)):
+            first_pass, count = UNITS[n]
             ready = ahead
-            more = g + 1 < CHUNKS
+            more = n + 1 < len(UNITS)
             if more:
-                turn_w(g + 1)
-                grouped_ahead = [turn_x(x_raw) for x_raw in x_raw_chunks[g + 1]]
-                quantise_w(g + 1)
+                next_pass, next_count = UNITS[n + 1]
+                opens_chunk = next_pass % PASSES_PER_CHUNK == 0
+                if opens_chunk:
+                    turn_w(next_pass // PASSES_PER_CHUNK)
+                grouped_ahead = [turn_x(x_raw, next_count) for x_raw in x_raw_units[n + 1]]
+                if opens_chunk:
+                    quantise_w(next_pass // PASSES_PER_CHUNK)
                 ahead = []
-            sums_ready = [multiply(g, ready[t][0], ready[t][1]) for t in range(BATCH_TILES)]
+            sums_ready = [
+                multiply(first_pass, count, ready[t][0], ready[t][1]) for t in range(BATCH_TILES)
+            ]
             for t in range(BATCH_TILES):
                 if more:
-                    ahead.append(quantise_x(grouped_ahead[t]))
-                add_and_store(g, t, sums_ready[t])
+                    ahead.append(quantise_x(grouped_ahead[t], next_count))
+                add_and_store(first_pass, count, t, sums_ready[t])

@@ -32,8 +32,11 @@ PLANE_1_SHIFT = PLANE_ROWS - PLANE_1_ROW
 ZERO_SHIFT = 40
 HOLD_BACK = 8
 
-UNITS = [(first, PASSES_PER_CHUNK) for first in range(0, PASSES - PASSES_PER_CHUNK, PASSES_PER_CHUNK)]
-UNITS = UNITS + [(PASSES - 4, 2), (PASSES - 2, 1), (PASSES - 1, 1)]
+UNITS = CHUNKS * BATCH_TILES
+LOOKAHEAD = 2
+
+WARM_UP_PASSES = 2
+IDLE_PASSES = 2
 
 
 FLOPS = 2 * BATCH * OUTS * 64
@@ -52,17 +55,38 @@ def tile_locallayer_k_kernel(tc, x, W, b, mask, out):
     nc = tc.nc
     with ExitStack() as ctx:
         const = ctx.enter_context(tc.tile_pool(name="const", bufs=1))
-        x_raw_pool = ctx.enter_context(tc.tile_pool(name="x_raw", bufs=len(UNITS) * BATCH_TILES))
+        x_raw_pool = ctx.enter_context(tc.tile_pool(name="x_raw", bufs=CHUNKS * BATCH_TILES))
         grouped_pool = ctx.enter_context(tc.tile_pool(name="grouped", bufs=2 * BATCH_TILES))
         x_mx_pool = ctx.enter_context(tc.tile_pool(name="x_mx", bufs=2 * BATCH_TILES))
         planes_psum = ctx.enter_context(tc.psum_pool(name="planes", bufs=5))
-        sums_psum = ctx.enter_context(tc.psum_pool(name="sums", bufs=3))
+        sums_psum = ctx.enter_context(tc.psum_pool(name="sums", bufs=2))
+        idle_psum = ctx.enter_context(tc.psum_pool(name="idle", bufs=1))
         ctx.enter_context(tc.manual_schedule())
 
         identity = const.tile([P, P], F32)
         make_identity(nc, identity[:])
         bias_rows = const.tile([P, OUTS], BF16)
         nc.vector.memset(bias_rows[:].bitcast(I32), 0)
+        zeros = const.tile([P, 4 * BANK], BF16, align_bytes=64)
+        zero_codes = const.tile([P, BANK], U32, align_bytes=64)
+        zero_scales = const.tile([P, BANK], U8, align_bytes=64)
+        nc.vector.memset(zeros[:].bitcast(I32), 0)
+        nc.vector.quantize_mx(out=zero_codes[:].bitcast(FP8X4), scales=zero_scales[:], in_=zeros[:])
+        idle_sums = idle_psum.tile([P, BANK], F32)
+
+        def idle_passes(count):
+            for n in range(count):
+                nc.tensor.matmul_mx(
+                    out=idle_sums[:],
+                    lhsT=zero_codes[:, 0:P].bitcast(FP8X4),
+                    lhsT_scale=zero_scales[:, 0:P],
+                    rhs=zero_codes[:].bitcast(FP8X4),
+                    rhs_scale=zero_scales[:],
+                    start=True,
+                    stop=True,
+                )
+
+        idle_passes(WARM_UP_PASSES)
         ones = const.tile([P, P], BF16)
         nc.vector.memset(ones[:], 1.0)
         w_raw = const.tile([P, PASSES, PLANE_K], BF16)
@@ -84,13 +108,12 @@ def tile_locallayer_k_kernel(tc, x, W, b, mask, out):
         w_codes = const.tile([P, PASSES * P], U32, align_bytes=64)
         w_scales = const.tile([P, PASSES * P], U8, align_bytes=64)
 
-        def load_x(first_pass, count, t):
+        def load_x(g, t):
             x_raw = x_raw_pool.tile([P, CHUNK_K], BF16)
-            for i in range(0, count, 2):
-                here = min(2, count - i)
+            for first in range(0, CHUNK_K, CHUNK_K // 2):
                 nc.sync.dma_start(
-                    out=x_raw[:, i * K_PASS : (i + here) * K_PASS],
-                    in_=x[t * P : (t + 1) * P, (first_pass + i) * K_PASS : (first_pass + i + here) * K_PASS],
+                    out=x_raw[:, first : first + CHUNK_K // 2],
+                    in_=x[t * P : (t + 1) * P, g * CHUNK_K + first : g * CHUNK_K + first + CHUNK_K // 2],
                 )
             return x_raw
 
@@ -121,43 +144,37 @@ def tile_locallayer_k_kernel(tc, x, W, b, mask, out):
 
         nc.sync.dma_start(out=bias_rows[0:1, :], in_=b.unsqueeze(0))
         x_raw_units = []
-        for first_pass, count in UNITS:
-            if first_pass % PASSES_PER_CHUNK == 0 and first_pass > 0:
-                load_w(first_pass // PASSES_PER_CHUNK)
-            x_raw_units.append([load_x(first_pass, count, t) for t in range(BATCH_TILES)])
-            if first_pass == 0:
-                load_w(0)
+        for g in range(CHUNKS):
+            for t in range(BATCH_TILES):
+                if t == 0:
+                    load_w(g)
+                x_raw_units.append(load_x(g, t))
 
-        def turn_x(x_raw, count):
+        def turn_x(x_raw):
             x_words = x_raw[:].bitcast(F32)
             grouped = grouped_pool.tile([P, CHUNK_K], BF16, align_bytes=64)
             grouped_words = grouped[:].bitcast(F32).rearrange(
                 "p (i r u) -> p i r u", i=PASSES_PER_CHUNK, u=PLANES
             )
             passes_per_bank = BANK // (PLANES * P)
-            for first in range(0, count, passes_per_bank):
-                here = min(passes_per_bank, count - first)
+            for first_pass in range(0, PASSES_PER_CHUNK, passes_per_bank):
                 planes = planes_psum.tile([P, passes_per_bank, PLANES, P], F32, tag="planes")
-                for i in range(here):
+                for i in range(passes_per_bank):
                     for u in range(PLANES):
-                        first_word = ((first + i) * PLANES + u) * P
+                        first_word = ((first_pass + i) * PLANES + u) * P
                         nc.tensor.transpose(
                             planes[:, i, u, :], x_words[:, first_word : first_word + P], identity[:]
                         )
                 nc.scalar.copy(
-                    out=grouped_words[:, first : first + here],
-                    in_=planes[:, 0:here].rearrange("p i u r -> p i r u"),
+                    out=grouped_words[:, first_pass : first_pass + passes_per_bank],
+                    in_=planes[:].rearrange("p i u r -> p i r u"),
                 )
             return grouped
 
-        def quantise_x(grouped, count):
+        def quantise_x(grouped):
             x_codes = x_mx_pool.tile([P, PASSES_PER_CHUNK * P], U32, align_bytes=64)
             x_scales = x_mx_pool.tile([P, PASSES_PER_CHUNK * P], U8, align_bytes=64)
-            nc.vector.quantize_mx(
-                out=x_codes[:, 0 : count * P].bitcast(FP8X4),
-                scales=x_scales[:, 0 : count * P],
-                in_=grouped[:, 0 : count * K_PASS],
-            )
+            nc.vector.quantize_mx(out=x_codes[:].bitcast(FP8X4), scales=x_scales[:], in_=grouped[:])
             return x_codes, x_scales
 
         def turn_w(g):
@@ -188,10 +205,10 @@ def tile_locallayer_k_kernel(tc, x, W, b, mask, out):
                 in_=w_grouped[:, g * CHUNK_K : (g + 1) * CHUNK_K],
             )
 
-        def multiply(first_pass, count, x_codes, x_scales):
+        def multiply(g, x_codes, x_scales):
             sums = sums_psum.tile([P, BANK], F32)
-            for i in range(count):
-                c = first_pass + i
+            for i in range(PASSES_PER_CHUNK):
+                c = g * PASSES_PER_CHUNK + i
                 nc.tensor.matmul_mx(
                     out=sums[:, i * P : (i + 1) * P],
                     lhsT=x_codes[:, i * P : (i + 1) * P].bitcast(FP8X4),
@@ -203,20 +220,17 @@ def tile_locallayer_k_kernel(tc, x, W, b, mask, out):
                 )
             return sums
 
-        def add_and_store(first_pass, count, t, sums):
+        def add_and_store(g, t, sums):
             windows = sums[:].rearrange("p (j two n) -> p j two n", two=2, n=P)
-            for parity in range(min(2, count)):
-                pairs = (count + 1) // 2
-                start = (first_pass + parity) * WINDOW_STEP
-                target = results[t][:, start : start + pairs * P].rearrange(
+            for parity in range(2):
+                first = (g * PASSES_PER_CHUNK + parity) * WINDOW_STEP
+                target = results[t][:, first : first + BANK // 2].rearrange(
                     "p (j n) -> p j n", n=P
                 )[:, :, 0:LIVE]
-                nc.vector.tensor_add(
-                    out=target, in0=windows[:, 0:pairs, parity, 0:LIVE], in1=target
-                )
-            stored = max(first_pass * WINDOW_STEP - HOLD_BACK, 0)
-            after = first_pass + count
-            complete = OUTS if after == PASSES else after * WINDOW_STEP - HOLD_BACK
+                nc.vector.tensor_add(out=target, in0=windows[:, :, parity, 0:LIVE], in1=target)
+            chunk_outs = PASSES_PER_CHUNK * WINDOW_STEP
+            stored = max(g * chunk_outs - HOLD_BACK, 0)
+            complete = OUTS if g == CHUNKS - 1 else (g + 1) * chunk_outs - HOLD_BACK
             nc.sync.dma_start(
                 out=out[t * P : (t + 1) * P, stored:complete],
                 in_=results[t][:, LEAD + stored : LEAD + complete],
@@ -233,28 +247,21 @@ def tile_locallayer_k_kernel(tc, x, W, b, mask, out):
                     out=results[t][:, LEAD + first : LEAD + first + BANK], in_=sums[:]
                 )
 
-        grouped_ahead = [turn_x(x_raw, UNITS[0][1]) for x_raw in x_raw_units[0]]
-        ahead = [quantise_x(grouped, UNITS[0][1]) for grouped in grouped_ahead]
-        turn_w(0)
-        quantise_w(0)
-
-        for n in range(len(UNITS)):
-            first_pass, count = UNITS[n]
-            ready = ahead
-            more = n + 1 < len(UNITS)
-            if more:
-                next_pass, next_count = UNITS[n + 1]
-                opens_chunk = next_pass % PASSES_PER_CHUNK == 0
-                if opens_chunk:
-                    turn_w(next_pass // PASSES_PER_CHUNK)
-                grouped_ahead = [turn_x(x_raw, next_count) for x_raw in x_raw_units[n + 1]]
-                if opens_chunk:
-                    quantise_w(next_pass // PASSES_PER_CHUNK)
-                ahead = []
-            sums_ready = [
-                multiply(first_pass, count, ready[t][0], ready[t][1]) for t in range(BATCH_TILES)
-            ]
-            for t in range(BATCH_TILES):
-                if more:
-                    ahead.append(quantise_x(grouped_ahead[t], next_count))
-                add_and_store(first_pass, count, t, sums_ready[t])
+        grouped_units = []
+        operands = []
+        for s in range(UNITS + LOOKAHEAD):
+            if s < UNITS:
+                if s % BATCH_TILES == 0:
+                    turn_w(s // BATCH_TILES)
+                grouped_units.append(turn_x(x_raw_units[s]))
+            if s >= LOOKAHEAD:
+                done = s - LOOKAHEAD
+                sums = multiply(done // BATCH_TILES, operands[done][0], operands[done][1])
+            if s < UNITS:
+                idle_passes(IDLE_PASSES)
+            if 1 <= s <= UNITS:
+                operands.append(quantise_x(grouped_units[s - 1]))
+                if (s - 1) % BATCH_TILES == 0:
+                    quantise_w((s - 1) // BATCH_TILES)
+            if s >= LOOKAHEAD:
+                add_and_store(done // BATCH_TILES, done % BATCH_TILES, sums)

@@ -25,18 +25,13 @@ BANK = 512
 WINDOW_STEP = 64
 LEAD = 2
 LIVE = 70
+CHUNK_LIVE = (PASSES_PER_CHUNK - 1) * WINDOW_STEP + LIVE
 PLACED = 72
 PLANE_ROWS = P // PLANES
 PLANE_1_ROW = PLACED - PLANE_ROWS
 PLANE_1_SHIFT = PLANE_ROWS - PLANE_1_ROW
 ZERO_SHIFT = 40
 HOLD_BACK = 8
-
-UNITS = CHUNKS * BATCH_TILES
-LOOKAHEAD = 2
-
-WARM_UP_PASSES = 2
-IDLE_PASSES = 2
 
 
 FLOPS = 2 * BATCH * OUTS * 64
@@ -59,34 +54,13 @@ def tile_locallayer_k_kernel(tc, x, W, b, mask, out):
         grouped_pool = ctx.enter_context(tc.tile_pool(name="grouped", bufs=2 * BATCH_TILES))
         x_mx_pool = ctx.enter_context(tc.tile_pool(name="x_mx", bufs=2 * BATCH_TILES))
         planes_psum = ctx.enter_context(tc.psum_pool(name="planes", bufs=5))
-        sums_psum = ctx.enter_context(tc.psum_pool(name="sums", bufs=2))
-        idle_psum = ctx.enter_context(tc.psum_pool(name="idle", bufs=1))
+        sums_psum = ctx.enter_context(tc.psum_pool(name="sums", bufs=3))
         ctx.enter_context(tc.manual_schedule())
 
         identity = const.tile([P, P], F32)
         make_identity(nc, identity[:])
         bias_rows = const.tile([P, OUTS], BF16)
         nc.vector.memset(bias_rows[:].bitcast(I32), 0)
-        zeros = const.tile([P, 4 * BANK], BF16, align_bytes=64)
-        zero_codes = const.tile([P, BANK], U32, align_bytes=64)
-        zero_scales = const.tile([P, BANK], U8, align_bytes=64)
-        nc.vector.memset(zeros[:].bitcast(I32), 0)
-        nc.vector.quantize_mx(out=zero_codes[:].bitcast(FP8X4), scales=zero_scales[:], in_=zeros[:])
-        idle_sums = idle_psum.tile([P, BANK], F32)
-
-        def idle_passes(count):
-            for n in range(count):
-                nc.tensor.matmul_mx(
-                    out=idle_sums[:],
-                    lhsT=zero_codes[:, 0:P].bitcast(FP8X4),
-                    lhsT_scale=zero_scales[:, 0:P],
-                    rhs=zero_codes[:].bitcast(FP8X4),
-                    rhs_scale=zero_scales[:],
-                    start=True,
-                    stop=True,
-                )
-
-        idle_passes(WARM_UP_PASSES)
         ones = const.tile([P, P], BF16)
         nc.vector.memset(ones[:], 1.0)
         w_raw = const.tile([P, PASSES, PLANE_K], BF16)
@@ -100,6 +74,11 @@ def tile_locallayer_k_kernel(tc, x, W, b, mask, out):
         for t in range(BATCH_TILES):
             nc.vector.memset(results[t][:, 0:LEAD], 0.0)
             nc.vector.memset(results[t][:, LEAD + OUTS :], 0.0)
+        zeros = const.tile([P, K_PASS], BF16, align_bytes=64)
+        zero_codes = const.tile([P, P], U32, align_bytes=64)
+        zero_scales = const.tile([P, P], U8, align_bytes=64)
+        nc.vector.memset(zeros[:].bitcast(I32), 0)
+        nc.vector.quantize_mx(out=zero_codes[:].bitcast(FP8X4), scales=zero_scales[:], in_=zeros[:])
         w_grouped = const.tile([P, PASSES * K_PASS], BF16, align_bytes=64)
         w_grouped_words = w_grouped[:].bitcast(F32).rearrange(
             "p (c n u) -> p c n u", c=PASSES, u=PLANES
@@ -143,12 +122,11 @@ def tile_locallayer_k_kernel(tc, x, W, b, mask, out):
                 )
 
         nc.sync.dma_start(out=bias_rows[0:1, :], in_=b.unsqueeze(0))
-        x_raw_units = []
-        for g in range(CHUNKS):
-            for t in range(BATCH_TILES):
-                if t == 0:
-                    load_w(g)
-                x_raw_units.append(load_x(g, t))
+        x_raw_chunks = [[load_x(0, t) for t in range(BATCH_TILES)]]
+        load_w(0)
+        for g in range(1, CHUNKS):
+            load_w(g)
+            x_raw_chunks.append([load_x(g, t) for t in range(BATCH_TILES)])
 
         def turn_x(x_raw):
             x_words = x_raw[:].bitcast(F32)
@@ -207,27 +185,28 @@ def tile_locallayer_k_kernel(tc, x, W, b, mask, out):
 
         def multiply(g, x_codes, x_scales):
             sums = sums_psum.tile([P, BANK], F32)
-            for i in range(PASSES_PER_CHUNK):
+            even = range(0, PASSES_PER_CHUNK + 1, 2)
+            odd = range(1, PASSES_PER_CHUNK, 2)
+            order = list(even) + list(odd)
+            for i in order:
                 c = g * PASSES_PER_CHUNK + i
+                marks_only = i == PASSES_PER_CHUNK
+                stationary = 0 if marks_only else i
                 nc.tensor.matmul_mx(
-                    out=sums[:, i * P : (i + 1) * P],
-                    lhsT=x_codes[:, i * P : (i + 1) * P].bitcast(FP8X4),
-                    lhsT_scale=x_scales[:, i * P : (i + 1) * P],
-                    rhs=w_codes[:, c * P : (c + 1) * P].bitcast(FP8X4),
-                    rhs_scale=w_scales[:, c * P : (c + 1) * P],
-                    start=True,
-                    stop=True,
+                    out=sums[:, i * WINDOW_STEP : i * WINDOW_STEP + P],
+                    lhsT=x_codes[:, stationary * P : (stationary + 1) * P].bitcast(FP8X4),
+                    lhsT_scale=x_scales[:, stationary * P : (stationary + 1) * P],
+                    rhs=(zero_codes[:] if marks_only else w_codes[:, c * P : (c + 1) * P]).bitcast(FP8X4),
+                    rhs_scale=zero_scales[:] if marks_only else w_scales[:, c * P : (c + 1) * P],
+                    start=(i == order[0]),
+                    stop=(i == order[-1]),
                 )
             return sums
 
         def add_and_store(g, t, sums):
-            windows = sums[:].rearrange("p (j two n) -> p j two n", two=2, n=P)
-            for parity in range(2):
-                first = (g * PASSES_PER_CHUNK + parity) * WINDOW_STEP
-                target = results[t][:, first : first + BANK // 2].rearrange(
-                    "p (j n) -> p j n", n=P
-                )[:, :, 0:LIVE]
-                nc.vector.tensor_add(out=target, in0=windows[:, :, parity, 0:LIVE], in1=target)
+            first = g * PASSES_PER_CHUNK * WINDOW_STEP
+            target = results[t][:, first : first + CHUNK_LIVE]
+            nc.vector.tensor_add(out=target, in0=sums[:, 0:CHUNK_LIVE], in1=target)
             chunk_outs = PASSES_PER_CHUNK * WINDOW_STEP
             stored = max(g * chunk_outs - HOLD_BACK, 0)
             complete = OUTS if g == CHUNKS - 1 else (g + 1) * chunk_outs - HOLD_BACK
@@ -247,21 +226,21 @@ def tile_locallayer_k_kernel(tc, x, W, b, mask, out):
                     out=results[t][:, LEAD + first : LEAD + first + BANK], in_=sums[:]
                 )
 
-        grouped_units = []
-        operands = []
-        for s in range(UNITS + LOOKAHEAD):
-            if s < UNITS:
-                if s % BATCH_TILES == 0:
-                    turn_w(s // BATCH_TILES)
-                grouped_units.append(turn_x(x_raw_units[s]))
-            if s >= LOOKAHEAD:
-                done = s - LOOKAHEAD
-                sums = multiply(done // BATCH_TILES, operands[done][0], operands[done][1])
-            if s < UNITS:
-                idle_passes(IDLE_PASSES)
-            if 1 <= s <= UNITS:
-                operands.append(quantise_x(grouped_units[s - 1]))
-                if (s - 1) % BATCH_TILES == 0:
-                    quantise_w((s - 1) // BATCH_TILES)
-            if s >= LOOKAHEAD:
-                add_and_store(done // BATCH_TILES, done % BATCH_TILES, sums)
+        grouped_ahead = [turn_x(x_raw) for x_raw in x_raw_chunks[0]]
+        ahead = [quantise_x(grouped) for grouped in grouped_ahead]
+        turn_w(0)
+        quantise_w(0)
+
+        for g in range(CHUNKS):
+            ready = ahead
+            more = g + 1 < CHUNKS
+            if more:
+                turn_w(g + 1)
+                grouped_ahead = [turn_x(x_raw) for x_raw in x_raw_chunks[g + 1]]
+                quantise_w(g + 1)
+                ahead = []
+            sums_ready = [multiply(g, ready[t][0], ready[t][1]) for t in range(BATCH_TILES)]
+            for t in range(BATCH_TILES):
+                if more:
+                    ahead.append(quantise_x(grouped_ahead[t]))
+                add_and_store(g, t, sums_ready[t])

@@ -121,7 +121,7 @@ def tile_locallayer_k_kernel(tc, x, W, b, mask, out):
                     ),
                 )
 
-        nc.sync.dma_start(out=bias_rows[0:1, :], in_=b.unsqueeze(0))
+        nc.scalar.dma_start(out=bias_rows[0:1, :], in_=b.unsqueeze(0))
         x_raw_chunks = [[load_x(0, t) for t in range(BATCH_TILES)]]
         load_w(0)
         for g in range(1, CHUNKS):

@@ -32,6 +32,8 @@ PLANE_1_ROW = PLACED - PLANE_ROWS
 PLANE_1_SHIFT = PLANE_ROWS - PLANE_1_ROW
 ZERO_SHIFT = 40
 HOLD_BACK = 8
+LAG = 2
+CARRIED = LIVE - WINDOW_STEP
 
 
 FLOPS = 2 * BATCH * OUTS * 64
@@ -68,12 +70,12 @@ def tile_locallayer_k_kernel(tc, x, W, b, mask, out):
         nc.vector.memset(w_raw[0:LEAD, 0, :], 0.0)
         nc.vector.memset(w_raw[P - 32 : P, last, :], 0.0)
         result_cols = WINDOW_STEP * last + P
+        bias = const.tile([P, result_cols], F32)
+        nc.vector.memset(bias[:, 0:LEAD], 0.0)
+        nc.vector.memset(bias[:, LEAD + OUTS :], 0.0)
         results = [
             const.tile([P, result_cols], F32, name="result_%d" % t) for t in range(BATCH_TILES)
         ]
-        for t in range(BATCH_TILES):
-            nc.vector.memset(results[t][:, 0:LEAD], 0.0)
-            nc.vector.memset(results[t][:, LEAD + OUTS :], 0.0)
         zeros = const.tile([P, K_PASS], BF16, align_bytes=64)
         zero_codes = const.tile([P, P], U32, align_bytes=64)
         zero_scales = const.tile([P, P], U8, align_bytes=64)
@@ -122,11 +124,14 @@ def tile_locallayer_k_kernel(tc, x, W, b, mask, out):
                 )
 
         nc.scalar.dma_start(out=bias_rows[0:1, :], in_=b.unsqueeze(0))
-        x_raw_chunks = [[load_x(0, t) for t in range(BATCH_TILES)]]
-        load_w(0)
-        for g in range(1, CHUNKS):
-            load_w(g)
-            x_raw_chunks.append([load_x(g, t) for t in range(BATCH_TILES)])
+        x_raw_units = []
+        for g in range(CHUNKS):
+            if g > 0:
+                load_w(g)
+            for t in range(BATCH_TILES):
+                x_raw_units.append(load_x(g, t))
+                if g == 0 and t == 0:
+                    load_w(0)
 
         def turn_x(x_raw):
             x_words = x_raw[:].bitcast(F32)
@@ -205,8 +210,15 @@ def tile_locallayer_k_kernel(tc, x, W, b, mask, out):
 
         def add_and_store(g, t, sums):
             first = g * PASSES_PER_CHUNK * WINDOW_STEP
-            target = results[t][:, first : first + CHUNK_LIVE]
-            nc.vector.tensor_add(out=target, in0=sums[:, 0:CHUNK_LIVE], in1=target)
+            carried = 0 if g == 0 else CARRIED
+            if carried:
+                target = results[t][:, first : first + carried]
+                nc.vector.tensor_add(out=target, in0=sums[:, 0:carried], in1=target)
+            nc.vector.tensor_add(
+                out=results[t][:, first + carried : first + CHUNK_LIVE],
+                in0=sums[:, carried:CHUNK_LIVE],
+                in1=bias[:, first + carried : first + CHUNK_LIVE],
+            )
             chunk_outs = PASSES_PER_CHUNK * WINDOW_STEP
             stored = max(g * chunk_outs - HOLD_BACK, 0)
             complete = OUTS if g == CHUNKS - 1 else (g + 1) * chunk_outs - HOLD_BACK
@@ -215,32 +227,33 @@ def tile_locallayer_k_kernel(tc, x, W, b, mask, out):
                 in_=results[t][:, LEAD + stored : LEAD + complete],
             )
 
-        for first in range(0, OUTS, BANK):
-            sums = sums_psum.tile([P, BANK], F32)
-            nc.tensor.matmul(
-                out=sums[:], lhsT=ones[:], rhs=bias_rows[:, first : first + BANK],
-                start=True, stop=True,
-            )
-            for t in range(BATCH_TILES):
-                nc.vector.tensor_copy(
-                    out=results[t][:, LEAD + first : LEAD + first + BANK], in_=sums[:]
+        def spread_bias():
+            for first in range(0, OUTS, BANK):
+                sums = sums_psum.tile([P, BANK], F32)
+                nc.tensor.matmul(
+                    out=sums[:], lhsT=ones[:], rhs=bias_rows[:, first : first + BANK],
+                    start=True, stop=True,
                 )
+                nc.vector.tensor_copy(out=bias[:, LEAD + first : LEAD + first + BANK], in_=sums[:])
 
-        grouped_ahead = [turn_x(x_raw) for x_raw in x_raw_chunks[0]]
-        ahead = [quantise_x(grouped) for grouped in grouped_ahead]
-        turn_w(0)
-        quantise_w(0)
+        def finish(g, t, operands):
+            add_and_store(g, t, multiply(g, *operands))
 
-        for g in range(CHUNKS):
-            ready = ahead
-            more = g + 1 < CHUNKS
-            if more:
-                turn_w(g + 1)
-                grouped_ahead = [turn_x(x_raw) for x_raw in x_raw_chunks[g + 1]]
-                quantise_w(g + 1)
-                ahead = []
-            sums_ready = [multiply(g, ready[t][0], ready[t][1]) for t in range(BATCH_TILES)]
-            for t in range(BATCH_TILES):
-                if more:
-                    ahead.append(quantise_x(grouped_ahead[t]))
-                add_and_store(g, t, sums_ready[t])
+        units = [(g, t) for g in range(CHUNKS) for t in range(BATCH_TILES)]
+        unfinished = []
+        for g, t in units:
+            if t == 0 and g > 0:
+                turn_w(g)
+                quantise_w(g)
+            grouped = turn_x(x_raw_units[g * BATCH_TILES + t])
+            if t == 0 and g == 0:
+                turn_w(g)
+            unfinished.append((g, t, quantise_x(grouped)))
+            if t == 0 and g == 0:
+                spread_bias()
+                quantise_w(g)
+            if len(unfinished) > LAG:
+                finish(*unfinished[0])
+                unfinished = unfinished[1:]
+        for unit in unfinished:
+            finish(*unit)

@@ -15,7 +15,6 @@ BATCH, FEATURES, OUTS = 256, 8192, 1024
 BATCH_TILES = BATCH // P
 K_PASS = 4 * P
 PLANES = 2
-PLANE_K = K_PASS // PLANES
 PASSES = FEATURES // K_PASS
 PASSES_PER_CHUNK = 4
 CHUNKS = PASSES // PASSES_PER_CHUNK
@@ -26,13 +25,18 @@ WINDOW_STEP = 64
 LEAD = 2
 LIVE = 70
 CHUNK_LIVE = (PASSES_PER_CHUNK - 1) * WINDOW_STEP + LIVE
+GROUP = 16
+GROUPS = WINDOW_STEP // GROUP
+GROUP_K = GROUP // 2 * 16
+STRIP_LEAD = 32
+STRIP = STRIP_LEAD + GROUP_K + 16
+PAIRS = PASSES // 2
+SLOT_WORDS = K_PASS // 2
+MARGIN = P
+ROOM = MARGIN + GROUPS * SLOT_WORDS + MARGIN
 PLACED = 72
-PLANE_ROWS = P // PLANES
-PLANE_1_ROW = PLACED - PLANE_ROWS
-PLANE_1_SHIFT = PLANE_ROWS - PLANE_1_ROW
-ZERO_SHIFT = 40
 HOLD_BACK = 8
-LAG = 2
+LAG = 3
 CARRIED = LIVE - WINDOW_STEP
 
 
@@ -40,12 +44,12 @@ FLOPS = 2 * BATCH * OUTS * 64
 BYTES = 2 * BATCH * FEATURES + 2 * OUTS * 64 + 2 * OUTS + 4 * BATCH * OUTS
 
 
-def diagonal_blocks(W, first_row, first_col, count):
-    block_step = WINDOW_STEP * FEATURES + K_PASS
-    start = first_row * FEATURES + first_col
-    flat = W.rearrange("o k -> (o k)")[start : start + count * block_step]
-    blocks = flat.rearrange("(j s) -> j s", s=block_step)[:, 0 : PLANE_ROWS * FEATURES]
-    return blocks.rearrange("j (r k) -> r j k", k=FEATURES)[:, :, 0:PLANE_K]
+def diagonal_strips(W, first, count):
+    step = GROUP * FEATURES + GROUP_K
+    start = first * step - STRIP_LEAD
+    flat = W.rearrange("o k -> (o k)")[start : start + count * step]
+    strips = flat.rearrange("(n s) -> n s", s=step)[:, 0 : GROUP * FEATURES]
+    return strips.rearrange("n (r k) -> r n k", k=FEATURES)[:, :, 0:STRIP]
 
 
 def tile_locallayer_k_kernel(tc, x, W, b, mask, out):
@@ -53,8 +57,8 @@ def tile_locallayer_k_kernel(tc, x, W, b, mask, out):
     with ExitStack() as ctx:
         const = ctx.enter_context(tc.tile_pool(name="const", bufs=1))
         x_raw_pool = ctx.enter_context(tc.tile_pool(name="x_raw", bufs=CHUNKS * BATCH_TILES))
-        grouped_pool = ctx.enter_context(tc.tile_pool(name="grouped", bufs=2 * BATCH_TILES))
-        x_mx_pool = ctx.enter_context(tc.tile_pool(name="x_mx", bufs=2 * BATCH_TILES))
+        grouped_pool = ctx.enter_context(tc.tile_pool(name="grouped", bufs=CHUNKS * BATCH_TILES))
+        x_mx_pool = ctx.enter_context(tc.tile_pool(name="x_mx", bufs=CHUNKS * BATCH_TILES))
         planes_psum = ctx.enter_context(tc.psum_pool(name="planes", bufs=5))
         sums_psum = ctx.enter_context(tc.psum_pool(name="sums", bufs=3))
         ctx.enter_context(tc.manual_schedule())
@@ -65,11 +69,19 @@ def tile_locallayer_k_kernel(tc, x, W, b, mask, out):
         nc.vector.memset(bias_rows[:].bitcast(I32), 0)
         ones = const.tile([P, P], BF16)
         nc.vector.memset(ones[:], 1.0)
-        w_raw = const.tile([P, PASSES, PLANE_K], BF16)
-        last = PASSES - 1
-        nc.vector.memset(w_raw[0:LEAD, 0, :], 0.0)
-        nc.vector.memset(w_raw[P - 32 : P, last, :], 0.0)
-        result_cols = WINDOW_STEP * last + P
+        w_raw = const.tile([P, 2 * 2 * ROOM], BF16)
+        w_words = w_raw[:].bitcast(F32)
+        strip_step = SLOT_WORDS + GROUP_K // 2
+        strip_start = MARGIN - STRIP_LEAD // 2
+        strip_end = strip_start + STRIP // 2
+        last_strip_end = strip_end + (2 * GROUPS - 1) * strip_step
+        nc.vector.memset(w_words[:, 0:MARGIN], 0.0)
+        nc.vector.memset(w_words[:, last_strip_end - 8 :], 0.0)
+        gaps = w_words[:, strip_end : strip_end + (2 * GROUPS - 1) * strip_step]
+        gaps = gaps.rearrange("p (s e) -> p s e", e=strip_step)[:, :, 0 : strip_step - STRIP // 2]
+        nc.vector.memset(gaps[:, 0:GROUPS, :], 0.0)
+        nc.gpsimd.memset(gaps[:, GROUPS:, :], 0.0)
+        result_cols = WINDOW_STEP * (PASSES - 1) + P
         bias = const.tile([P, result_cols], F32)
         nc.vector.memset(bias[:, 0:LEAD], 0.0)
         nc.vector.memset(bias[:, LEAD + OUTS :], 0.0)
@@ -83,55 +95,53 @@ def tile_locallayer_k_kernel(tc, x, W, b, mask, out):
         nc.vector.quantize_mx(out=zero_codes[:].bitcast(FP8X4), scales=zero_scales[:], in_=zeros[:])
         w_grouped = const.tile([P, PASSES * K_PASS], BF16, align_bytes=64)
         w_grouped_words = w_grouped[:].bitcast(F32).rearrange(
-            "p (c n u) -> p c n u", c=PASSES, u=PLANES
+            "p (q h n u) -> p q h n u", h=2, n=P, u=PLANES
         )
-        nc.gpsimd.memset(w_grouped_words[:, :, PLACED:, :], 0.0)
+        nc.gpsimd.memset(w_grouped_words[:, :, :, PLACED:, :], 0.0)
+        nc.vector.memset(w_grouped_words[:, 0, 0, 0:LEAD, :], 0.0)
+        nc.vector.memset(w_grouped_words[:, PAIRS - 1, 1, LEAD + WINDOW_STEP : PLACED, :], 0.0)
         w_codes = const.tile([P, PASSES * P], U32, align_bytes=64)
         w_scales = const.tile([P, PASSES * P], U8, align_bytes=64)
 
-        def load_x(g, t):
+        def load_x(g, t, pieces):
             x_raw = x_raw_pool.tile([P, CHUNK_K], BF16)
-            for first in range(0, CHUNK_K, CHUNK_K // 2):
+            width = CHUNK_K // pieces
+            for first in range(0, CHUNK_K, width):
                 nc.sync.dma_start(
-                    out=x_raw[:, first : first + CHUNK_K // 2],
-                    in_=x[t * P : (t + 1) * P, g * CHUNK_K + first : g * CHUNK_K + first + CHUNK_K // 2],
+                    out=x_raw[:, first : first + width],
+                    in_=x[t * P : (t + 1) * P, g * CHUNK_K + first : g * CHUNK_K + first + width],
                 )
             return x_raw
 
-        def load_w(g):
-            first = g * PASSES_PER_CHUNK
-            if g == 0:
+        def load_w(q):
+            rows = w_raw[q:P:PAIRS, :].rearrange("p (s e) -> p s e", e=2 * strip_step)
+            first = 2 * GROUPS * q
+            lo, hi = 0, 2 * GROUPS
+            if q == 0:
+                lo = 1
                 nc.sync.dma_start(
-                    out=w_raw[LEAD:PLANE_ROWS, 0, :], in_=W[0 : PLANE_ROWS - LEAD, 0:PLANE_K]
+                    out=rows[:, 0, 2 * MARGIN : 2 * strip_end], in_=W[0:GROUP, 0 : STRIP - STRIP_LEAD]
                 )
-            if g == CHUNKS - 1:
-                last_row = WINDOW_STEP * last - LEAD + PLANE_1_ROW
+            if q == PAIRS - 1:
+                hi -= 1
                 nc.sync.dma_start(
-                    out=w_raw[PLANE_ROWS : PLANE_ROWS + OUTS - last_row, last, :],
-                    in_=W[last_row:OUTS, FEATURES - PLANE_K : FEATURES],
+                    out=rows[:, hi, 2 * strip_start : 2 * strip_end - 16],
+                    in_=W[OUTS - GROUP : OUTS, FEATURES - STRIP + 16 : FEATURES],
                 )
-            for u in range(PLANES):
-                lo = max(first, 1) if u == 0 else first
-                hi = first + PASSES_PER_CHUNK if u == 0 else min(first + PASSES_PER_CHUNK, last)
-                nc.sync.dma_start(
-                    out=w_raw[u * PLANE_ROWS : (u + 1) * PLANE_ROWS, lo:hi, :],
-                    in_=diagonal_blocks(
-                        W,
-                        WINDOW_STEP * lo - LEAD + u * PLANE_1_ROW,
-                        K_PASS * lo + u * PLANE_K,
-                        hi - lo,
-                    ),
-                )
+            nc.sync.dma_start(
+                out=rows[:, lo:hi, 2 * strip_start : 2 * strip_end],
+                in_=diagonal_strips(W, first + lo, hi - lo),
+            )
 
         nc.scalar.dma_start(out=bias_rows[0:1, :], in_=b.unsqueeze(0))
+        units = [(g, t) for g in range(CHUNKS) for t in range(BATCH_TILES)]
         x_raw_units = []
-        for g in range(CHUNKS):
-            if g > 0:
-                load_w(g)
-            for t in range(BATCH_TILES):
-                x_raw_units.append(load_x(g, t))
-                if g == 0 and t == 0:
-                    load_w(0)
+        for unit in units:
+            pieces = 2 if unit in (units[0], units[-1]) else 1
+            x_raw_units.append(load_x(unit[0], unit[1], pieces))
+            if unit == units[1]:
+                for q in range(PAIRS):
+                    load_w(q)
 
         def turn_x(x_raw):
             x_words = x_raw[:].bitcast(F32)
@@ -160,26 +170,44 @@ def tile_locallayer_k_kernel(tc, x, W, b, mask, out):
             nc.vector.quantize_mx(out=x_codes[:].bitcast(FP8X4), scales=x_scales[:], in_=grouped[:])
             return x_codes, x_scales
 
-        def turn_w(g):
-            w_words = w_raw[:].bitcast(F32)
-            passes = slice(g * PASSES_PER_CHUNK, (g + 1) * PASSES_PER_CHUNK)
-            turned = planes_psum.tile([P, PASSES_PER_CHUNK, P], F32, tag="planes")
-            for i in range(PASSES_PER_CHUNK):
-                nc.tensor.transpose(
-                    turned[:, i, :], w_words[:, g * PASSES_PER_CHUNK + i, :], identity[:]
+        def turn_w():
+            def window(h, group, u):
+                first = h * ROOM + MARGIN + group * SLOT_WORDS + u * P
+                return w_words[:, first : first + P]
+
+            def turn(windows):
+                turned = planes_psum.tile([P, 4, P], F32, tag="planes")
+                for i in range(len(windows)):
+                    nc.tensor.transpose(turned[:, i, :], window(*windows[i]), identity[:])
+                return turned
+
+            def place(copy, turned, first, rows, pairs, h, n):
+                r0, r1 = rows
+                q0, q1 = pairs
+                source = turned[:, first : first + PLANES, :].rearrange("p u (r q) -> p q r u", q=PAIRS)
+                copy(
+                    out=w_grouped_words[:, q0 + n[0] : q1 + n[0], h, n[1] : n[1] + r1 - r0, :],
+                    in_=source[:, q0:q1, r0:r1, :],
                 )
-            nc.scalar.copy(
-                out=w_grouped_words[:, passes, 0:PLANE_1_SHIFT, :],
-                in_=turned[:, :, 0 : PLANES * PLANE_1_SHIFT].rearrange(
-                    "p i (u n) -> p i n u", u=PLANES
-                ),
-            )
-            nc.scalar.copy(
-                out=w_grouped_words[:, passes, PLANE_1_SHIFT:PLACED, :],
-                in_=turned[:, :, P - PLANES * ZERO_SHIFT : P].rearrange(
-                    "p i (u n) -> p i n u", u=PLANES
-                )[:, :, ZERO_SHIFT - (PLACED - PLANE_1_SHIFT) : ZERO_SHIFT, :],
-            )
+
+            all_rows = (0, GROUP)
+            all_pairs = (0, PAIRS)
+            for h, copy in ((0, nc.scalar.copy), (1, nc.vector.tensor_copy)):
+                turned = turn([(h, 0, 0), (h, 0, 1), (h, 3, 1)])
+                place(copy, turned, 0, all_rows, all_pairs, h, (0, LEAD))
+                place(copy, turned, 1, all_rows, all_pairs, h, (0, LEAD + 3 * GROUP))
+                turned = turn([(h, 1, 0), (h, 1, 1), (h, 2, 0), (h, 2, 1)])
+                place(copy, turned, 0, all_rows, all_pairs, h, (0, LEAD + GROUP))
+                place(copy, turned, 2, all_rows, all_pairs, h, (0, LEAD + 2 * GROUP))
+            copy = nc.vector.tensor_copy
+            turned = turn([(0, 3, 2), (0, 0, -1), (1, 3, 2), (1, 0, -1)])
+            before = LEAD + WINDOW_STEP
+            upper = (GROUP - LEAD, GROUP)
+            lower = (0, PLACED - before)
+            place(copy, turned, 0, upper, all_pairs, 1, (0, 0))
+            place(copy, turned, 2, upper, (0, PAIRS - 1), 0, (1, 0))
+            place(copy, turned, 2, lower, all_pairs, 0, (0, before))
+            place(copy, turned, 0, lower, (1, PAIRS), 1, (-1, before))
 
         def quantise_w(g):
             nc.vector.quantize_mx(
@@ -234,23 +262,21 @@ def tile_locallayer_k_kernel(tc, x, W, b, mask, out):
                     out=sums[:], lhsT=ones[:], rhs=bias_rows[:, first : first + BANK],
                     start=True, stop=True,
                 )
-                nc.vector.tensor_copy(out=bias[:, LEAD + first : LEAD + first + BANK], in_=sums[:])
+                nc.scalar.copy(out=bias[:, LEAD + first : LEAD + first + BANK], in_=sums[:])
 
         def finish(g, t, operands):
             add_and_store(g, t, multiply(g, *operands))
 
-        units = [(g, t) for g in range(CHUNKS) for t in range(BATCH_TILES)]
         unfinished = []
         for g, t in units:
-            if t == 0 and g > 0:
-                turn_w(g)
-                quantise_w(g)
             grouped = turn_x(x_raw_units[g * BATCH_TILES + t])
-            if t == 0 and g == 0:
-                turn_w(g)
             unfinished.append((g, t, quantise_x(grouped)))
-            if t == 0 and g == 0:
+            if (g, t) == units[0]:
                 spread_bias()
+            if (g, t) == units[1]:
+                turn_w()
+                quantise_w(0)
+            if t == 0 and g > 0:
                 quantise_w(g)
             if len(unfinished) > LAG:
                 finish(*unfinished[0])

@@ -16,15 +16,14 @@ BATCH_TILES = BATCH // P
 K_PASS = 4 * P
 PLANES = 2
 PASSES = FEATURES // K_PASS
-PASSES_PER_CHUNK = 4
-CHUNKS = PASSES // PASSES_PER_CHUNK
-CHUNK_K = PASSES_PER_CHUNK * K_PASS
 BANK = 512
+CHUNK = 4
+CHUNKS = PASSES // CHUNK
+W_PASSES = 8
 
 WINDOW_STEP = 64
 LEAD = 2
 LIVE = 70
-CHUNK_LIVE = (PASSES_PER_CHUNK - 1) * WINDOW_STEP + LIVE
 GROUP = 16
 GROUPS = WINDOW_STEP // GROUP
 GROUP_K = GROUP // 2 * 16
@@ -36,8 +35,6 @@ MARGIN = P
 ROOM = MARGIN + GROUPS * SLOT_WORDS + MARGIN
 PLACED = 72
 HOLD_BACK = 8
-LAG = 3
-CARRIED = LIVE - WINDOW_STEP
 
 
 FLOPS = 2 * BATCH * OUTS * 64
@@ -58,35 +55,40 @@ def tile_locallayer_k_kernel(tc, x, W, b, mask, out):
         const = ctx.enter_context(tc.tile_pool(name="const", bufs=1))
         x_raw_pool = ctx.enter_context(tc.tile_pool(name="x_raw", bufs=CHUNKS * BATCH_TILES))
         grouped_pool = ctx.enter_context(tc.tile_pool(name="grouped", bufs=CHUNKS * BATCH_TILES))
-        x_mx_pool = ctx.enter_context(tc.tile_pool(name="x_mx", bufs=CHUNKS * BATCH_TILES))
-        planes_psum = ctx.enter_context(tc.psum_pool(name="planes", bufs=5))
-        sums_psum = ctx.enter_context(tc.psum_pool(name="sums", bufs=3))
+        staged_pool = ctx.enter_context(tc.tile_pool(name="staged", bufs=CHUNKS * BATCH_TILES))
+        planes_psum = ctx.enter_context(tc.psum_pool(name="planes", bufs=4))
+        sums_psum = ctx.enter_context(tc.psum_pool(name="sums", bufs=4))
         ctx.enter_context(tc.manual_schedule())
 
-        identity = const.tile([P, P], F32)
-        make_identity(nc, identity[:])
-        bias_rows = const.tile([P, OUTS], BF16)
-        nc.vector.memset(bias_rows[:].bitcast(I32), 0)
-        ones = const.tile([P, P], BF16)
-        nc.vector.memset(ones[:], 1.0)
+        spare = const.tile([P, 1], F32)
+        nc.vector.memset(spare[:], 0.0)
+        nc.scalar.copy(out=spare[:], in_=spare[:])
         w_raw = const.tile([P, 2 * 2 * ROOM], BF16)
         w_words = w_raw[:].bitcast(F32)
         strip_step = SLOT_WORDS + GROUP_K // 2
         strip_start = MARGIN - STRIP_LEAD // 2
         strip_end = strip_start + STRIP // 2
         last_strip_end = strip_end + (2 * GROUPS - 1) * strip_step
-        nc.vector.memset(w_words[:, 0:MARGIN], 0.0)
-        nc.vector.memset(w_words[:, last_strip_end - 8 :], 0.0)
         gaps = w_words[:, strip_end : strip_end + (2 * GROUPS - 1) * strip_step]
         gaps = gaps.rearrange("p (s e) -> p s e", e=strip_step)[:, :, 0 : strip_step - STRIP // 2]
         nc.vector.memset(gaps[:, 0:GROUPS, :], 0.0)
+        nc.gpsimd.memset(w_words[:, 0:MARGIN], 0.0)
         nc.gpsimd.memset(gaps[:, GROUPS:, :], 0.0)
-        result_cols = WINDOW_STEP * (PASSES - 1) + P
-        bias = const.tile([P, result_cols], F32)
-        nc.vector.memset(bias[:, 0:LEAD], 0.0)
-        nc.vector.memset(bias[:, LEAD + OUTS :], 0.0)
-        results = [
-            const.tile([P, result_cols], F32, name="result_%d" % t) for t in range(BATCH_TILES)
+        nc.gpsimd.memset(w_words[:, last_strip_end - 8 :], 0.0)
+        identity = const.tile([P, P], F32)
+        make_identity(nc, identity[:])
+        bias_rows = const.tile([P, OUTS], BF16)
+        nc.vector.memset(bias_rows[:].bitcast(I32), 0)
+        ones = const.tile([P, P], BF16)
+        nc.vector.memset(ones[:], 1.0)
+        bias = const.tile([P, OUTS], F32)
+        x_codes = [
+            const.tile([P, PASSES * P], U32, align_bytes=64, name="x_codes_%d" % t)
+            for t in range(BATCH_TILES)
+        ]
+        x_scales = [
+            const.tile([P, PASSES * P], U8, align_bytes=64, name="x_scales_%d" % t)
+            for t in range(BATCH_TILES)
         ]
         zeros = const.tile([P, K_PASS], BF16, align_bytes=64)
         zero_codes = const.tile([P, P], U32, align_bytes=64)
@@ -104,12 +106,13 @@ def tile_locallayer_k_kernel(tc, x, W, b, mask, out):
         w_scales = const.tile([P, PASSES * P], U8, align_bytes=64)
 
         def load_x(g, t, pieces):
-            x_raw = x_raw_pool.tile([P, CHUNK_K], BF16)
-            width = CHUNK_K // pieces
-            for first in range(0, CHUNK_K, width):
+            x_raw = x_raw_pool.tile([P, CHUNK * K_PASS], BF16)
+            width = CHUNK * K_PASS // pieces
+            for first in range(0, CHUNK * K_PASS, width):
+                col = g * CHUNK * K_PASS + first
                 nc.sync.dma_start(
                     out=x_raw[:, first : first + width],
-                    in_=x[t * P : (t + 1) * P, g * CHUNK_K + first : g * CHUNK_K + first + width],
+                    in_=x[t * P : (t + 1) * P, col : col + width],
                 )
             return x_raw
 
@@ -135,22 +138,21 @@ def tile_locallayer_k_kernel(tc, x, W, b, mask, out):
 
         nc.scalar.dma_start(out=bias_rows[0:1, :], in_=b.unsqueeze(0))
         units = [(g, t) for g in range(CHUNKS) for t in range(BATCH_TILES)]
-        x_raw_units = []
+        x_raw_units = {}
         for unit in units:
-            pieces = 2 if unit in (units[0], units[-1]) else 1
-            x_raw_units.append(load_x(unit[0], unit[1], pieces))
-            if unit == units[1]:
+            x_raw_units[unit] = load_x(unit[0], unit[1], 2 if unit in (units[0], units[-1]) else 1)
+            if unit == units[0]:
                 for q in range(PAIRS):
                     load_w(q)
 
         def turn_x(x_raw):
             x_words = x_raw[:].bitcast(F32)
-            grouped = grouped_pool.tile([P, CHUNK_K], BF16, align_bytes=64)
+            grouped = grouped_pool.tile([P, CHUNK * K_PASS], BF16, align_bytes=64)
             grouped_words = grouped[:].bitcast(F32).rearrange(
-                "p (i r u) -> p i r u", i=PASSES_PER_CHUNK, u=PLANES
+                "p (i r u) -> p i r u", i=CHUNK, u=PLANES
             )
             passes_per_bank = BANK // (PLANES * P)
-            for first_pass in range(0, PASSES_PER_CHUNK, passes_per_bank):
+            for first_pass in range(0, CHUNK, passes_per_bank):
                 planes = planes_psum.tile([P, passes_per_bank, PLANES, P], F32, tag="planes")
                 for i in range(passes_per_bank):
                     for u in range(PLANES):
@@ -164,11 +166,15 @@ def tile_locallayer_k_kernel(tc, x, W, b, mask, out):
                 )
             return grouped
 
-        def quantise_x(grouped):
-            x_codes = x_mx_pool.tile([P, PASSES_PER_CHUNK * P], U32, align_bytes=64)
-            x_scales = x_mx_pool.tile([P, PASSES_PER_CHUNK * P], U8, align_bytes=64)
-            nc.vector.quantize_mx(out=x_codes[:].bitcast(FP8X4), scales=x_scales[:], in_=grouped[:])
-            return x_codes, x_scales
+        def quantise_x(g, t, grouped, pieces):
+            passes = CHUNK // pieces
+            for i in range(0, CHUNK, passes):
+                cols = slice((g * CHUNK + i) * P, (g * CHUNK + i + passes) * P)
+                nc.vector.quantize_mx(
+                    out=x_codes[t][:, cols].bitcast(FP8X4),
+                    scales=x_scales[t][:, cols],
+                    in_=grouped[:, i * K_PASS : (i + passes) * K_PASS],
+                )
 
         def turn_w():
             def window(h, group, u):
@@ -192,10 +198,13 @@ def tile_locallayer_k_kernel(tc, x, W, b, mask, out):
 
             all_rows = (0, GROUP)
             all_pairs = (0, PAIRS)
-            for h, copy in ((0, nc.scalar.copy), (1, nc.vector.tensor_copy)):
+            for h in range(2):
+                copy = nc.scalar.copy
                 turned = turn([(h, 0, 0), (h, 0, 1), (h, 3, 1)])
                 place(copy, turned, 0, all_rows, all_pairs, h, (0, LEAD))
                 place(copy, turned, 1, all_rows, all_pairs, h, (0, LEAD + 3 * GROUP))
+                if h == 1:
+                    copy = nc.vector.tensor_copy
                 turned = turn([(h, 1, 0), (h, 1, 1), (h, 2, 0), (h, 2, 1)])
                 place(copy, turned, 0, all_rows, all_pairs, h, (0, LEAD + GROUP))
                 place(copy, turned, 2, all_rows, all_pairs, h, (0, LEAD + 2 * GROUP))
@@ -209,51 +218,44 @@ def tile_locallayer_k_kernel(tc, x, W, b, mask, out):
             place(copy, turned, 2, lower, all_pairs, 0, (0, before))
             place(copy, turned, 0, lower, (1, PAIRS), 1, (-1, before))
 
-        def quantise_w(g):
+        def quantise_w(first):
+            cols = slice(first * P, (first + W_PASSES) * P)
             nc.vector.quantize_mx(
-                out=w_codes[:, g * CHUNK_K // 4 : (g + 1) * CHUNK_K // 4].bitcast(FP8X4),
-                scales=w_scales[:, g * CHUNK_K // 4 : (g + 1) * CHUNK_K // 4],
-                in_=w_grouped[:, g * CHUNK_K : (g + 1) * CHUNK_K],
+                out=w_codes[:, cols].bitcast(FP8X4),
+                scales=w_scales[:, cols],
+                in_=w_grouped[:, first * K_PASS : (first + W_PASSES) * K_PASS],
             )
 
-        def multiply(g, x_codes, x_scales):
+        def multiply(g, t):
             sums = sums_psum.tile([P, BANK], F32)
-            even = range(0, PASSES_PER_CHUNK + 1, 2)
-            odd = range(1, PASSES_PER_CHUNK, 2)
-            order = list(even) + list(odd)
+            first = max(g * CHUNK - 1, 0)
+            order = list(range(0, CHUNK + 1, 2)) + list(range(1, CHUNK, 2))
             for i in order:
-                c = g * PASSES_PER_CHUNK + i
-                marks_only = i == PASSES_PER_CHUNK
-                stationary = 0 if marks_only else i
+                on_zeros = g == 0 and i == CHUNK
+                x_pass = slice(first * P, (first + 1) * P)
+                w_pass = slice((first + i) * P, (first + i + 1) * P)
+                if not on_zeros:
+                    x_pass = w_pass
                 nc.tensor.matmul_mx(
                     out=sums[:, i * WINDOW_STEP : i * WINDOW_STEP + P],
-                    lhsT=x_codes[:, stationary * P : (stationary + 1) * P].bitcast(FP8X4),
-                    lhsT_scale=x_scales[:, stationary * P : (stationary + 1) * P],
-                    rhs=(zero_codes[:] if marks_only else w_codes[:, c * P : (c + 1) * P]).bitcast(FP8X4),
-                    rhs_scale=zero_scales[:] if marks_only else w_scales[:, c * P : (c + 1) * P],
+                    lhsT=x_codes[t][:, x_pass].bitcast(FP8X4),
+                    lhsT_scale=x_scales[t][:, x_pass],
+                    rhs=(zero_codes[:] if on_zeros else w_codes[:, w_pass]).bitcast(FP8X4),
+                    rhs_scale=zero_scales[:] if on_zeros else w_scales[:, w_pass],
                     start=(i == order[0]),
                     stop=(i == order[-1]),
                 )
             return sums
 
         def add_and_store(g, t, sums):
-            first = g * PASSES_PER_CHUNK * WINDOW_STEP
-            carried = 0 if g == 0 else CARRIED
-            if carried:
-                target = results[t][:, first : first + carried]
-                nc.vector.tensor_add(out=target, in0=sums[:, 0:carried], in1=target)
+            lo = max(g * CHUNK * WINDOW_STEP - HOLD_BACK, 0)
+            hi = OUTS if g == CHUNKS - 1 else (g + 1) * CHUNK * WINDOW_STEP - HOLD_BACK
+            start = max(g * CHUNK - 1, 0) * WINDOW_STEP - LEAD
+            staged = staged_pool.tile([P, CHUNK * WINDOW_STEP + HOLD_BACK], F32)
             nc.vector.tensor_add(
-                out=results[t][:, first + carried : first + CHUNK_LIVE],
-                in0=sums[:, carried:CHUNK_LIVE],
-                in1=bias[:, first + carried : first + CHUNK_LIVE],
+                out=staged[:, 0 : hi - lo], in0=sums[:, lo - start : hi - start], in1=bias[:, lo:hi]
             )
-            chunk_outs = PASSES_PER_CHUNK * WINDOW_STEP
-            stored = max(g * chunk_outs - HOLD_BACK, 0)
-            complete = OUTS if g == CHUNKS - 1 else (g + 1) * chunk_outs - HOLD_BACK
-            nc.sync.dma_start(
-                out=out[t * P : (t + 1) * P, stored:complete],
-                in_=results[t][:, LEAD + stored : LEAD + complete],
-            )
+            nc.sync.dma_start(out=out[t * P : (t + 1) * P, lo:hi], in_=staged[:, 0 : hi - lo])
 
         def spread_bias():
             for first in range(0, OUTS, BANK):
@@ -262,24 +264,21 @@ def tile_locallayer_k_kernel(tc, x, W, b, mask, out):
                     out=sums[:], lhsT=ones[:], rhs=bias_rows[:, first : first + BANK],
                     start=True, stop=True,
                 )
-                nc.scalar.copy(out=bias[:, LEAD + first : LEAD + first + BANK], in_=sums[:])
+                nc.scalar.copy(out=bias[:, first : first + BANK], in_=sums[:])
 
-        def finish(g, t, operands):
-            add_and_store(g, t, multiply(g, *operands))
-
-        unfinished = []
-        for g, t in units:
-            grouped = turn_x(x_raw_units[g * BATCH_TILES + t])
-            unfinished.append((g, t, quantise_x(grouped)))
-            if (g, t) == units[0]:
-                spread_bias()
-            if (g, t) == units[1]:
-                turn_w()
-                quantise_w(0)
-            if t == 0 and g > 0:
-                quantise_w(g)
-            if len(unfinished) > LAG:
-                finish(*unfinished[0])
-                unfinished = unfinished[1:]
-        for unit in unfinished:
-            finish(*unit)
+        for g in range(CHUNKS + 1):
+            if g < CHUNKS:
+                for t in range(BATCH_TILES):
+                    grouped = turn_x(x_raw_units[(g, t)])
+                    if (g, t) == units[0]:
+                        spread_bias()
+                    quantise_x(g, t, grouped, 2 if (g, t) == units[-1] else 1)
+                    if (g, t) == units[0]:
+                        turn_w()
+                        quantise_w(0)
+                if g == 0:
+                    quantise_w(W_PASSES)
+            if g > 0:
+                sums_ready = [multiply(g - 1, t) for t in range(BATCH_TILES)]
+                for t in range(BATCH_TILES):
+                    add_and_store(g - 1, t, sums_ready[t])

@@ -19,7 +19,7 @@ PASSES = FEATURES // K_PASS
 BANK = 512
 CHUNK = 4
 CHUNKS = PASSES // CHUNK
-W_PASSES = 8
+W_PASSES = 4
 
 WINDOW_STEP = 64
 LEAD = 2
@@ -34,6 +34,7 @@ SLOT_WORDS = K_PASS // 2
 MARGIN = P
 ROOM = MARGIN + GROUPS * SLOT_WORDS + MARGIN
 PLACED = 72
+LAG = 3
 HOLD_BACK = 8
 
 
@@ -145,7 +146,7 @@ def tile_locallayer_k_kernel(tc, x, W, b, mask, out):
                 for q in range(PAIRS):
                     load_w(q)
 
-        def turn_x(x_raw):
+        def turn_x(x_raw, copies):
             x_words = x_raw[:].bitcast(F32)
             grouped = grouped_pool.tile([P, CHUNK * K_PASS], BF16, align_bytes=64)
             grouped_words = grouped[:].bitcast(F32).rearrange(
@@ -160,7 +161,7 @@ def tile_locallayer_k_kernel(tc, x, W, b, mask, out):
                         nc.tensor.transpose(
                             planes[:, i, u, :], x_words[:, first_word : first_word + P], identity[:]
                         )
-                nc.scalar.copy(
+                copies[first_pass // passes_per_bank](
                     out=grouped_words[:, first_pass : first_pass + passes_per_bank],
                     in_=planes[:].rearrange("p i u r -> p i r u"),
                 )
@@ -208,7 +209,7 @@ def tile_locallayer_k_kernel(tc, x, W, b, mask, out):
                 turned = turn([(h, 1, 0), (h, 1, 1), (h, 2, 0), (h, 2, 1)])
                 place(copy, turned, 0, all_rows, all_pairs, h, (0, LEAD + GROUP))
                 place(copy, turned, 2, all_rows, all_pairs, h, (0, LEAD + 2 * GROUP))
-            copy = nc.vector.tensor_copy
+            copy = nc.scalar.copy
             turned = turn([(0, 3, 2), (0, 0, -1), (1, 3, 2), (1, 0, -1)])
             before = LEAD + WINDOW_STEP
             upper = (GROUP - LEAD, GROUP)
@@ -266,19 +267,20 @@ def tile_locallayer_k_kernel(tc, x, W, b, mask, out):
                 )
                 nc.scalar.copy(out=bias[:, first : first + BANK], in_=sums[:])
 
-        for g in range(CHUNKS + 1):
-            if g < CHUNKS:
-                for t in range(BATCH_TILES):
-                    grouped = turn_x(x_raw_units[(g, t)])
-                    if (g, t) == units[0]:
-                        spread_bias()
-                    quantise_x(g, t, grouped, 2 if (g, t) == units[-1] else 1)
-                    if (g, t) == units[0]:
-                        turn_w()
-                        quantise_w(0)
-                if g == 0:
-                    quantise_w(W_PASSES)
-            if g > 0:
-                sums_ready = [multiply(g - 1, t) for t in range(BATCH_TILES)]
-                for t in range(BATCH_TILES):
-                    add_and_store(g - 1, t, sums_ready[t])
+        unfinished = []
+        for g, t in units:
+            second = nc.vector.tensor_copy if (g, t) == units[0] else nc.scalar.copy
+            grouped = turn_x(x_raw_units[(g, t)], (nc.scalar.copy, second))
+            if (g, t) == units[0]:
+                spread_bias()
+            quantise_x(g, t, grouped, 2 if (g, t) == units[-1] else 1)
+            if (g, t) == units[0]:
+                turn_w()
+            if (g, t) in units[: PASSES // W_PASSES]:
+                quantise_w(units.index((g, t)) * W_PASSES)
+            unfinished.append((g, t))
+            if len(unfinished) > LAG:
+                add_and_store(*unfinished[0], multiply(*unfinished[0]))
+                unfinished = unfinished[1:]
+        for unit in unfinished:
+            add_and_store(*unit, multiply(*unit))

@@ -142,7 +142,7 @@ def tile_locallayer_k_kernel(tc, x, W, b, mask, out):
         x_raw_units = {}
         for unit in units:
             x_raw_units[unit] = load_x(unit[0], unit[1], 2 if unit in (units[0], units[-1]) else 1)
-            if unit == units[0]:
+            if unit == units[1]:
                 for q in range(PAIRS):
                     load_w(q)
 
@@ -271,13 +271,12 @@ def tile_locallayer_k_kernel(tc, x, W, b, mask, out):
         for g, t in units:
             second = nc.vector.tensor_copy if (g, t) == units[0] else nc.scalar.copy
             grouped = turn_x(x_raw_units[(g, t)], (nc.scalar.copy, second))
-            if (g, t) == units[0]:
-                spread_bias()
             quantise_x(g, t, grouped, 2 if (g, t) == units[-1] else 1)
-            if (g, t) == units[0]:
+            if (g, t) == units[1]:
+                spread_bias()
                 turn_w()
-            if (g, t) in units[: PASSES // W_PASSES]:
-                quantise_w(units.index((g, t)) * W_PASSES)
+            if (g, t) in units[1 : 1 + PASSES // W_PASSES]:
+                quantise_w((units.index((g, t)) - 1) * W_PASSES)
             unfinished.append((g, t))
             if len(unfinished) > LAG:
                 add_and_store(*unfinished[0], multiply(*unfinished[0]))

from contextlib import ExitStack

import concourse.mybir as mybir
from concourse.masks import make_identity

F32 = mybir.dt.float32
BF16 = mybir.dt.bfloat16
U32 = mybir.dt.uint32
U8 = mybir.dt.uint8
I32 = mybir.dt.int32
FP8X4 = mybir.dt.float8_e4m3fn_x4

P = 128
BATCH, FEATURES, OUTS = 256, 8192, 1024
BATCH_TILES = BATCH // P
K_PASS = 4 * P
PLANES = 2
PASSES = FEATURES // K_PASS
BANK = 512
CHUNK = 4
CHUNKS = PASSES // CHUNK
W_PASSES = 4

WINDOW_STEP = 64
LEAD = 2
LIVE = 70
GROUP = 16
GROUPS = WINDOW_STEP // GROUP
GROUP_K = GROUP // 2 * 16
STRIP_LEAD = 32
STRIP = STRIP_LEAD + GROUP_K + 16
PAIRS = PASSES // 2
SLOT_WORDS = K_PASS // 2
MARGIN = P
ROOM = MARGIN + GROUPS * SLOT_WORDS + MARGIN
PLACED = 72
LAG = 3
HOLD_BACK = 8


FLOPS = 2 * BATCH * OUTS * 64
BYTES = 2 * BATCH * FEATURES + 2 * OUTS * 64 + 2 * OUTS + 4 * BATCH * OUTS


def diagonal_strips(W, first, count):
    step = GROUP * FEATURES + GROUP_K
    start = first * step - STRIP_LEAD
    flat = W.rearrange("o k -> (o k)")[start : start + count * step]
    strips = flat.rearrange("(n s) -> n s", s=step)[:, 0 : GROUP * FEATURES]
    return strips.rearrange("n (r k) -> r n k", k=FEATURES)[:, :, 0:STRIP]


def tile_locallayer_k_kernel(tc, x, W, b, mask, out):
    nc = tc.nc
    with ExitStack() as ctx:
        const = ctx.enter_context(tc.tile_pool(name="const", bufs=1))
        x_raw_pool = ctx.enter_context(tc.tile_pool(name="x_raw", bufs=CHUNKS * BATCH_TILES))
        grouped_pool = ctx.enter_context(tc.tile_pool(name="grouped", bufs=CHUNKS * BATCH_TILES))
        staged_pool = ctx.enter_context(tc.tile_pool(name="staged", bufs=CHUNKS * BATCH_TILES))
        planes_psum = ctx.enter_context(tc.psum_pool(name="planes", bufs=4))
        sums_psum = ctx.enter_context(tc.psum_pool(name="sums", bufs=4))
        ctx.enter_context(tc.manual_schedule())

        spare = const.tile([P, 1], F32)
        nc.vector.memset(spare[:], 0.0)
        nc.scalar.copy(out=spare[:], in_=spare[:])
        w_raw = const.tile([P, 2 * 2 * ROOM], BF16)
        w_words = w_raw[:].bitcast(F32)
        strip_step = SLOT_WORDS + GROUP_K // 2
        strip_start = MARGIN - STRIP_LEAD // 2
        strip_end = strip_start + STRIP // 2
        last_strip_end = strip_end + (2 * GROUPS - 1) * strip_step
        gaps = w_words[:, strip_end : strip_end + (2 * GROUPS - 1) * strip_step]
        gaps = gaps.rearrange("p (s e) -> p s e", e=strip_step)[:, :, 0 : strip_step - STRIP // 2]
        nc.vector.memset(gaps[:, 0:GROUPS, :], 0.0)
        nc.gpsimd.memset(w_words[:, 0:MARGIN], 0.0)
        nc.gpsimd.memset(gaps[:, GROUPS:, :], 0.0)
        nc.gpsimd.memset(w_words[:, last_strip_end - 8 :], 0.0)
        identity = const.tile([P, P], F32)
        make_identity(nc, identity[:])
        bias_rows = const.tile([P, OUTS], BF16)
        nc.vector.memset(bias_rows[:].bitcast(I32), 0)
        ones = const.tile([P, P], BF16)
        nc.vector.memset(ones[:], 1.0)
        bias = const.tile([P, OUTS], F32)
        x_codes = [
            const.tile([P, PASSES * P], U32, align_bytes=64, name="x_codes_%d" % t)
            for t in range(BATCH_TILES)
        ]
        x_scales = [
            const.tile([P, PASSES * P], U8, align_bytes=64, name="x_scales_%d" % t)
            for t in range(BATCH_TILES)
        ]
        zeros = const.tile([P, K_PASS], BF16, align_bytes=64)
        zero_codes = const.tile([P, P], U32, align_bytes=64)
        zero_scales = const.tile([P, P], U8, align_bytes=64)
        nc.vector.memset(zeros[:].bitcast(I32), 0)
        nc.vector.quantize_mx(out=zero_codes[:].bitcast(FP8X4), scales=zero_scales[:], in_=zeros[:])
        w_grouped = const.tile([P, PASSES * K_PASS], BF16, align_bytes=64)
        w_grouped_words = w_grouped[:].bitcast(F32).rearrange(
            "p (q h n u) -> p q h n u", h=2, n=P, u=PLANES
        )
        nc.gpsimd.memset(w_grouped_words[:, :, :, PLACED:, :], 0.0)
        nc.vector.memset(w_grouped_words[:, 0, 0, 0:LEAD, :], 0.0)
        nc.vector.memset(w_grouped_words[:, PAIRS - 1, 1, LEAD + WINDOW_STEP : PLACED, :], 0.0)
        w_codes = const.tile([P, PASSES * P], U32, align_bytes=64)
        w_scales = const.tile([P, PASSES * P], U8, align_bytes=64)

        def load_x(g, t, pieces):
            x_raw = x_raw_pool.tile([P, CHUNK * K_PASS], BF16)
            width = CHUNK * K_PASS // pieces
            for first in range(0, CHUNK * K_PASS, width):
                col = g * CHUNK * K_PASS + first
                nc.sync.dma_start(
                    out=x_raw[:, first : first + width],
                    in_=x[t * P : (t + 1) * P, col : col + width],
                )
            return x_raw

        def load_w(q):
            rows = w_raw[q:P:PAIRS, :].rearrange("p (s e) -> p s e", e=2 * strip_step)
            first = 2 * GROUPS * q
            lo, hi = 0, 2 * GROUPS
            if q == 0:
                lo = 1
                nc.sync.dma_start(
                    out=rows[:, 0, 2 * MARGIN : 2 * strip_end], in_=W[0:GROUP, 0 : STRIP - STRIP_LEAD]
                )
            if q == PAIRS - 1:
                hi -= 1
                nc.sync.dma_start(
                    out=rows[:, hi, 2 * strip_start : 2 * strip_end - 16],
                    in_=W[OUTS - GROUP : OUTS, FEATURES - STRIP + 16 : FEATURES],
                )
            nc.sync.dma_start(
                out=rows[:, lo:hi, 2 * strip_start : 2 * strip_end],
                in_=diagonal_strips(W, first + lo, hi - lo),
            )

        nc.scalar.dma_start(out=bias_rows[0:1, :], in_=b.unsqueeze(0))
        units = [(g, t) for g in range(CHUNKS) for t in range(BATCH_TILES)]
        x_raw_units = {}
        for unit in units:
            x_raw_units[unit] = load_x(unit[0], unit[1], 2 if unit in (units[0], units[-1]) else 1)
            if unit == units[1]:
                for q in range(PAIRS):
                    load_w(q)

        def turn_x(x_raw, copies):
            x_words = x_raw[:].bitcast(F32)
            grouped = grouped_pool.tile([P, CHUNK * K_PASS], BF16, align_bytes=64)
            grouped_words = grouped[:].bitcast(F32).rearrange(
                "p (i r u) -> p i r u", i=CHUNK, u=PLANES
            )
            passes_per_bank = BANK // (PLANES * P)
            for first_pass in range(0, CHUNK, passes_per_bank):
                planes = planes_psum.tile([P, passes_per_bank, PLANES, P], F32, tag="planes")
                for i in range(passes_per_bank):
                    for u in range(PLANES):
                        first_word = ((first_pass + i) * PLANES + u) * P
                        nc.tensor.transpose(
                            planes[:, i, u, :], x_words[:, first_word : first_word + P], identity[:]
                        )
                copies[first_pass // passes_per_bank](
                    out=grouped_words[:, first_pass : first_pass + passes_per_bank],
                    in_=planes[:].rearrange("p i u r -> p i r u"),
                )
            return grouped

        def quantise_x(g, t, grouped, pieces):
            passes = CHUNK // pieces
            for i in range(0, CHUNK, passes):
                cols = slice((g * CHUNK + i) * P, (g * CHUNK + i + passes) * P)
                nc.vector.quantize_mx(
                    out=x_codes[t][:, cols].bitcast(FP8X4),
                    scales=x_scales[t][:, cols],
                    in_=grouped[:, i * K_PASS : (i + passes) * K_PASS],
                )

        def turn_w():
            def window(h, group, u):
                first = h * ROOM + MARGIN + group * SLOT_WORDS + u * P
                return w_words[:, first : first + P]

            def turn(windows):
                turned = planes_psum.tile([P, 4, P], F32, tag="planes")
                for i in range(len(windows)):
                    nc.tensor.transpose(turned[:, i, :], window(*windows[i]), identity[:])
                return turned

            def place(copy, turned, first, rows, pairs, h, n):
                r0, r1 = rows
                q0, q1 = pairs
                source = turned[:, first : first + PLANES, :].rearrange("p u (r q) -> p q r u", q=PAIRS)
                copy(
                    out=w_grouped_words[:, q0 + n[0] : q1 + n[0], h, n[1] : n[1] + r1 - r0, :],
                    in_=source[:, q0:q1, r0:r1, :],
                )

            all_rows = (0, GROUP)
            all_pairs = (0, PAIRS)
            for h in range(2):
                copy = nc.scalar.copy
                turned = turn([(h, 0, 0), (h, 0, 1), (h, 3, 1)])
                place(copy, turned, 0, all_rows, all_pairs, h, (0, LEAD))
                place(copy, turned, 1, all_rows, all_pairs, h, (0, LEAD + 3 * GROUP))
                if h == 1:
                    copy = nc.vector.tensor_copy
                turned = turn([(h, 1, 0), (h, 1, 1), (h, 2, 0), (h, 2, 1)])
                place(copy, turned, 0, all_rows, all_pairs, h, (0, LEAD + GROUP))
                place(copy, turned, 2, all_rows, all_pairs, h, (0, LEAD + 2 * GROUP))
            copy = nc.scalar.copy
            turned = turn([(0, 3, 2), (0, 0, -1), (1, 3, 2), (1, 0, -1)])
            before = LEAD + WINDOW_STEP
            upper = (GROUP - LEAD, GROUP)
            lower = (0, PLACED - before)
            place(copy, turned, 0, upper, all_pairs, 1, (0, 0))
            place(copy, turned, 2, upper, (0, PAIRS - 1), 0, (1, 0))
            place(copy, turned, 2, lower, all_pairs, 0, (0, before))
            place(copy, turned, 0, lower, (1, PAIRS), 1, (-1, before))

        def quantise_w(first):
            cols = slice(first * P, (first + W_PASSES) * P)
            nc.vector.quantize_mx(
                out=w_codes[:, cols].bitcast(FP8X4),
                scales=w_scales[:, cols],
                in_=w_grouped[:, first * K_PASS : (first + W_PASSES) * K_PASS],
            )

        def multiply(g, t):
            sums = sums_psum.tile([P, BANK], F32)
            first = max(g * CHUNK - 1, 0)
            order = list(range(0, CHUNK + 1, 2)) + list(range(1, CHUNK, 2))
            for i in order:
                on_zeros = g == 0 and i == CHUNK
                x_pass = slice(first * P, (first + 1) * P)
                w_pass = slice((first + i) * P, (first + i + 1) * P)
                if not on_zeros:
                    x_pass = w_pass
                nc.tensor.matmul_mx(
                    out=sums[:, i * WINDOW_STEP : i * WINDOW_STEP + P],
                    lhsT=x_codes[t][:, x_pass].bitcast(FP8X4),
                    lhsT_scale=x_scales[t][:, x_pass],
                    rhs=(zero_codes[:] if on_zeros else w_codes[:, w_pass]).bitcast(FP8X4),
                    rhs_scale=zero_scales[:] if on_zeros else w_scales[:, w_pass],
                    start=(i == order[0]),
                    stop=(i == order[-1]),
                )
            return sums

        def add_and_store(g, t, sums):
            lo = max(g * CHUNK * WINDOW_STEP - HOLD_BACK, 0)
            hi = OUTS if g == CHUNKS - 1 else (g + 1) * CHUNK * WINDOW_STEP - HOLD_BACK
            start = max(g * CHUNK - 1, 0) * WINDOW_STEP - LEAD
            staged = staged_pool.tile([P, CHUNK * WINDOW_STEP + HOLD_BACK], F32)
            nc.vector.tensor_add(
                out=staged[:, 0 : hi - lo], in0=sums[:, lo - start : hi - start], in1=bias[:, lo:hi]
            )
            nc.sync.dma_start(out=out[t * P : (t + 1) * P, lo:hi], in_=staged[:, 0 : hi - lo])

        def spread_bias():
            for first in range(0, OUTS, BANK):
                sums = sums_psum.tile([P, BANK], F32)
                nc.tensor.matmul(
                    out=sums[:], lhsT=ones[:], rhs=bias_rows[:, first : first + BANK],
                    start=True, stop=True,
                )
                nc.scalar.copy(out=bias[:, first : first + BANK], in_=sums[:])

        unfinished = []
        for g, t in units:
            second = nc.vector.tensor_copy if (g, t) == units[0] else nc.scalar.copy
            grouped = turn_x(x_raw_units[(g, t)], (nc.scalar.copy, second))
            quantise_x(g, t, grouped, 2 if (g, t) == units[-1] else 1)
            if (g, t) == units[1]:
                spread_bias()
                turn_w()
            if (g, t) in units[1 : 1 + PASSES // W_PASSES]:
                quantise_w((units.index((g, t)) - 1) * W_PASSES)
            unfinished.append((g, t))
            if len(unfinished) > LAG:
                add_and_store(*unfinished[0], multiply(*unfinished[0]))
                unfinished = unfinished[1:]
        for unit in unfinished:
            add_and_store(*unit, multiply(*unit))
